import numpy as np
import ml_dtypes


def mxq(x, axis, fmt="e4m3"):
    dtype, down = {"e4m3": (ml_dtypes.float8_e4m3fn, 7), "e5m2": (ml_dtypes.float8_e5m2, 14)}[fmt]
    v = np.moveaxis(np.asarray(x, np.float32).astype(ml_dtypes.bfloat16).astype(np.float64), axis, -1)
    blocks = v.reshape(v.shape[:-1] + (-1, 32))
    amax = np.abs(blocks).max(-1, keepdims=True)
    byte = np.maximum(np.where(amax > 0, np.frexp(amax)[1] - 1 + 127, 0) - down, 1)
    scale = np.exp2(byte - 127.0)
    codes = (blocks / scale).astype(np.float32).astype(dtype).astype(np.float64)
    return np.moveaxis((codes * scale).reshape(v.shape), -1, axis)


WIDE = False


def mx_kscale(k):
    if not WIDE:
        return np.ones(k)
    levels = np.array([10, -10, 5, -5, 0])
    a = np.random.permutation(np.resize(levels, k // 512 * 4)).reshape(k // 512, 4)
    idx = np.arange(k)
    return np.exp2(a[idx // 512, idx % 128 // 32])


BF16 = ml_dtypes.bfloat16


def bf(x):
    return np.asarray(x, np.float32).astype(BF16)


def f64(x):
    return np.asarray(x).astype(np.float64)


B, C, F, T, H, W = 2, 512, 8192, 4, 8, 8
N = T * H * W
BN_EPS = 1e-5


def setup_inputs():
    t = mx_kscale(F)
    return {"inputs": bf(np.random.standard_normal((B, C, T, H, W))),
            "Wv": bf(np.random.standard_normal((F, C)) / np.sqrt(C) * t[:, None]),
            "bv": bf(np.random.standard_normal(F) * 0.3 * t),
            "row": bf(1.0 + 0.1 * np.random.standard_normal((B, N))),
            "Wo": bf(np.random.standard_normal((C, F)) * 1.5 / np.sqrt(F) / t[None, :]),
            "bo": bf(np.random.standard_normal(C) * 0.3),
            "gamma": bf(1.0 + 0.1 * np.random.standard_normal(C)),
            "beta": bf(np.random.standard_normal(C) * 0.1)}


def reference(inputs, Wv, bv, row, Wo, bo, gamma, beta):
    x = f64(inputs).reshape(B, C, N)
    V = (mxq(f64(Wv), 1, "e4m3") @ mxq(x, 1, "e4m3")) + f64(bv)[None, :, None]
    V1 = np.maximum(V * f64(row)[:, None, :], 0.0)
    out = (mxq(f64(Wo), 1, "e4m3") @ mxq(V1, 1, "e4m3")) + f64(bo)[None, :, None]
    res = x + np.maximum(out, 0.0)
    mean = res.mean(axis=(0, -1), keepdims=True)
    var = res.var(axis=(0, -1), keepdims=True)
    xhat = (res - mean) / np.sqrt(var + BN_EPS)
    y = f64(gamma)[None, :, None] * xhat + f64(beta)[None, :, None]
    return y.reshape(B, C, T, H, W)

@@ -1,0 +1,263 @@
+from contextlib import ExitStack
+
+import concourse.masks as masks
+import concourse.mybir as mybir
+
+F32 = mybir.dt.float32
+BF16 = mybir.dt.bfloat16
+U32 = mybir.dt.uint32
+U8 = mybir.dt.uint8
+FP8X4 = mybir.dt.float8_e4m3fn_x4
+ALU = mybir.AluOpType
+ACT = mybir.ActivationFunctionType
+
+P = 128
+PACK = 4
+K_PASS = P * PACK
+B, C, F, N = 2, 512, 8192, 256
+BN = B * N
+GROUPS = F // K_PASS
+BN_EPS = 1e-5
+RUN = 4
+
+SCALAR_COLS = 448
+
+FLOPS = 2 * (2 * F * C * BN)
+
+
+def side_by_side(rows, grouped):
+    return (
+        rows.rearrange("p t (c i) -> p c t i", i=RUN),
+        grouped.rearrange("p (c i) t -> p c t i", i=RUN),
+    )
+
+
+def tile_nonlocallayer_pa_k_kernel(tc, inputs, Wv, bv, row, Wo, bo, gamma, beta, out):
+    nc = tc.nc
+    x_dram = inputs.rearrange("b c t h w -> b c (t h w)")
+    y_dram = out.rearrange("b c t h w -> b c (t h w)")
+
+    with ExitStack() as ctx:
+        const = ctx.enter_context(tc.tile_pool(name="const", bufs=1))
+        raw = ctx.enter_context(tc.tile_pool(name="raw", bufs=GROUPS))
+        work = ctx.enter_context(tc.tile_pool(name="work", bufs=2))
+        psum_t = ctx.enter_context(tc.psum_pool(name="psum_t", bufs=2))
+        psum_v = ctx.enter_context(tc.psum_pool(name="psum_v", bufs=2))
+        psum_o = ctx.enter_context(tc.psum_pool(name="psum_o", bufs=1))
+        ctx.enter_context(tc.manual_schedule())
+
+        def load_wv(g):
+            t = raw.tile([P, PACK, C], BF16, name="wv_raw")
+            nc.sync.dma_start(
+                out=t[:].rearrange("r (u e) c -> r u (e c)", e=2),
+                in_=Wv[g * K_PASS : (g + 1) * K_PASS, :].rearrange("(u r e) c -> r u (e c)", u=2, e=2),
+            )
+            return t
+
+        def load_wo(g):
+            t = raw.tile([P, PACK, K_PASS], BF16, name="wo_raw")
+            nc.sync.dma_start(
+                out=t[:], in_=Wo[:, g * K_PASS : (g + 1) * K_PASS].rearrange("(r t) f -> r t f", t=PACK)
+            )
+            return t
+
+        wv_raw = [load_wv(0)]
+        x_rows = const.tile([P, B, PACK, N], BF16)
+        for b in range(B):
+            nc.sync.dma_start(
+                out=x_rows[:, b].rearrange("p (h e) n -> p h (e n)", e=2),
+                in_=x_dram[b].rearrange("(h p e) n -> p h (e n)", h=2, e=2),
+            )
+        wo_raw = [load_wo(0)]
+        for g in range(1, GROUPS):
+            wv_raw.append(load_wv(g))
+            wo_raw.append(load_wo(g))
+        x_res = const.tile([P, B, PACK, N], BF16)
+        for b in range(B):
+            nc.sync.dma_start(
+                out=x_res[:, b].rearrange("p t n -> p (t n)"),
+                in_=x_dram[b].rearrange("(p t) n -> p (t n)", t=PACK),
+            )
+        chan_bf = const.tile([P, 3, 16], BF16)
+        for k, vec in enumerate((bo, gamma, beta)):
+            nc.sync.dma_start(out=chan_bf[:, k, 0:PACK], in_=vec.rearrange("(p t) -> p t", t=PACK))
+
+        eps = const.tile([P, 1], F32)
+        nc.vector.memset(eps[:], BN_EPS)
+
+        ident = const.tile([P, P], F32)
+        masks.make_identity(nc, ident[:])
+
+        bv_rows = const.tile([P, 2 * P], BF16)
+        nc.vector.memset(bv_rows[:], 0.0)
+        nc.scalar.dma_start(out=bv_rows[0 : 2 * GROUPS, :], in_=bv.rearrange("(j w) -> j w", w=2 * P))
+        row_one = const.tile([P, BN], BF16)
+        nc.vector.memset(row_one[:], 0.0)
+        nc.scalar.dma_start(out=row_one[0:1, :], in_=row.rearrange("b n -> (b n)").unsqueeze(0))
+        ones = const.tile([P, P], BF16)
+        nc.vector.memset(ones[:], 1.0)
+        warm = const.tile([P, 1], F32)
+        nc.scalar.activation(out=warm[:], in_=eps[:], func=ACT.Sqrt)
+
+        def transpose_weights(rows, name):
+            grouped = work.tile([P, PACK * P, 2], F32, name=name, align_bytes=64)
+            for j in range(2):
+                bank = psum_t.tile([P, 2, 2 * P], F32, name="bank_t")
+                for i in range(2):
+                    words = rows[:, 2 * j + i, :].bitcast(F32)
+                    for h in range(2):
+                        nc.tensor.transpose(
+                            bank[:, h, i * P : (i + 1) * P], words[:, h * P : (h + 1) * P], ident[:]
+                        )
+                nc.scalar.copy(
+                    out=grouped[:, 2 * j * P : 2 * (j + 1) * P, :], in_=bank[:].rearrange("p h c -> p c h")
+                )
+            return grouped
+
+        def quantise(values, width, name, bufs):
+            words = work.tile([P, width], U32, name=name + "_words", bufs=bufs, align_bytes=64)
+            scales = work.tile([P, width], U8, name=name + "_scales", bufs=bufs, align_bytes=64)
+            nc.vector.quantize_mx(out=words[:].bitcast(FP8X4), scales=scales[:], in_=values)
+            return words, scales
+
+        def quantise_weights(grouped, name, bufs):
+            return quantise(grouped[:].rearrange("p c h -> p (c h)").bitcast(BF16), PACK * P, name, bufs)
+
+        def first_matmul(g, tiles):
+            words, scales = wv_q[g]
+            for t in tiles:
+                cols = slice(t * P, (t + 1) * P)
+                bank = psum_v.tile([P, BN], F32, name="bank_v")
+                nc.tensor.matmul_mx(
+                    out=bank[:],
+                    lhsT=words[:, cols].bitcast(FP8X4),
+                    lhsT_scale=scales[:, cols],
+                    rhs=x_words[:].bitcast(FP8X4),
+                    rhs_scale=x_scales[:],
+                    start=True,
+                    stop=True,
+                )
+                nc.vector.scalar_tensor_tensor(
+                    out=gated[g][:, t, :],
+                    in0=bank[:],
+                    scalar=bv_f32[:, PACK * g + t : PACK * g + t + 1],
+                    in1=row_all[:],
+                    op0=ALU.add,
+                    op1=ALU.mult,
+                )
+
+        def second_matmul(g, tiles):
+            w_words, w_scales = wo_q[g]
+            v_words, v_scales = v1_q[g]
+            for t in tiles:
+                cols = slice(t * P, (t + 1) * P)
+                nc.tensor.matmul_mx(
+                    out=acc[t][:],
+                    lhsT=w_words[:, cols].bitcast(FP8X4),
+                    lhsT_scale=w_scales[:, cols],
+                    rhs=v_words[:].bitcast(FP8X4),
+                    rhs_scale=v_scales[:],
+                    start=(g == 0),
+                    stop=(g == GROUPS - 1),
+                )
+
+        def relu_regroup_scalar(g, first, last):
+            src, dst = side_by_side(gated[g][:, :, first:last], v1[g][:, first:last, :])
+            nc.scalar.activation(out=dst, in_=src, func=ACT.Relu)
+
+        def relu_regroup_vector(g, first, last):
+            src, dst = side_by_side(gated[g][:, :, first:last], v1[g][:, first:last, :])
+            nc.vector.tensor_scalar_max(out=dst, in0=src, scalar1=0.0)
+
+        wv_q, wo_q, v1_q, gated, v1 = {}, {}, {}, {}, {}
+        acc = [psum_o.tile([P, BN], F32, name="acc%d" % t) for t in range(PACK)]
+
+        wv_grouped = transpose_weights(wv_raw[0], "wv_grouped")
+
+        x_grouped = const.tile([P, B, N, PACK], BF16, align_bytes=64)
+        for b in range(B):
+            src, dst = side_by_side(x_rows[:, b], x_grouped[:, b])
+            nc.vector.tensor_copy(out=dst, in_=src)
+
+        bank = psum_v.tile([P, BN], F32, name="bank_v")
+        nc.tensor.transpose(bank[:, 0:P], bv_rows[:].bitcast(F32), ident[:])
+        bv_f32 = const.tile([P, PACK * GROUPS], F32)
+        nc.vector.tensor_copy(out=bv_f32[:], in_=bank[:, 0 : 2 * GROUPS].bitcast(BF16))
+
+        bank = psum_v.tile([P, BN], F32, name="bank_v")
+        nc.tensor.matmul(out=bank[:], lhsT=ones[:], rhs=row_one[:], start=True, stop=True)
+        row_all = const.tile([P, BN], F32)
+        nc.vector.tensor_copy(out=row_all[:], in_=bank[:])
+
+        x_words, x_scales = quantise(x_grouped[:].rearrange("p b n t -> p (b n t)"), BN, "x", 1)
+        wv_q[0] = quantise_weights(wv_grouped, "wv", 2)
+
+        half = SCALAR_COLS // 2
+        for i in range(GROUPS + 2):
+            if 0 <= i - 2:
+                v1_q[i - 2] = quantise(v1[i - 2][:].rearrange("p c t -> p (c t)"), BN, "v1", 2)
+            if i + 1 < GROUPS:
+                wv_grouped = transpose_weights(wv_raw[i + 1], "wv_grouped")
+            if i < GROUPS:
+                gated[i] = work.tile([P, PACK, BN], BF16, name="gated")
+                first_matmul(i, (0, 1))
+            if 0 <= i - 2:
+                second_matmul(i - 2, (0, 1))
+            if i + 1 < GROUPS:
+                wv_q[i + 1] = quantise_weights(wv_grouped, "wv", 2)
+            if 0 <= i - 1 < GROUPS:
+                v1[i - 1] = work.tile([P, BN, PACK], BF16, name="v1", align_bytes=64)
+                relu_regroup_scalar(i - 1, 0, half)
+                relu_regroup_vector(i - 1, SCALAR_COLS, BN)
+            if i < GROUPS:
+                wo_grouped = transpose_weights(wo_raw[i], "wo_grouped")
+                first_matmul(i, (2, 3))
+            if 0 <= i - 2:
+                second_matmul(i - 2, (2, 3))
+            if i < GROUPS:
+                wo_q[i] = quantise_weights(wo_grouped, "wo", 3)
+            if 0 <= i - 1 < GROUPS:
+                relu_regroup_scalar(i - 1, half, SCALAR_COLS)
+
+        chan = const.tile([P, 3, PACK], F32)
+        nc.vector.tensor_copy(out=chan[:], in_=chan_bf[:, :, 0:PACK])
+        res = const.tile([P, B, PACK, N], F32)
+        stats = const.tile([P, PACK, 6], F32)
+        mean_var = const.tile([P, PACK, 2], F32)
+        for t in range(PACK):
+            positive = work.tile([P, B, N], F32, name="positive")
+            nc.scalar.activation(
+                out=positive[:].rearrange("p b n -> p (b n)"), in_=acc[t][:], func=ACT.Relu, bias=chan[:, 0, t : t + 1]
+            )
+            nc.vector.tensor_tensor(out=res[:, :, t, :], in0=positive[:], in1=x_res[:, :, t, :], op=ALU.add)
+            nc.vector.bn_stats(out=stats[:, t, :], in_=res[:, :, t, :])
+            nc.vector.bn_aggr(out=mean_var[:, t, :], in_=stats[:, t, :])
+        gain = const.tile([P, PACK], F32)
+        shift = const.tile([P, PACK], F32)
+        nc.scalar.activation(out=gain[:], in_=mean_var[:, :, 1], func=ACT.Sqrt, bias=eps[:, 0:1])
+        nc.vector.reciprocal(out=gain[:], in_=gain[:])
+        nc.vector.tensor_tensor(out=gain[:], in0=gain[:], in1=chan[:, 1, :], op=ALU.mult)
+        nc.vector.tensor_tensor(out=shift[:], in0=mean_var[:, :, 0], in1=gain[:], op=ALU.mult)
+        nc.vector.tensor_tensor(out=shift[:], in0=chan[:, 2, :], in1=shift[:], op=ALU.subtract)
+        for t in range(PACK):
+            if t % 2 == 0:
+                nc.vector.tensor_scalar(
+                    out=res[:, :, t, :],
+                    in0=res[:, :, t, :],
+                    scalar1=gain[:, t : t + 1],
+                    scalar2=shift[:, t : t + 1],
+                    op0=ALU.mult,
+                    op1=ALU.add,
+                )
+            else:
+                nc.scalar.activation(
+                    out=res[:, :, t, :],
+                    in_=res[:, :, t, :],
+                    func=ACT.Identity,
+                    scale=gain[:, t : t + 1],
+                    bias=shift[:, t : t + 1],
+                )
+        for b in range(B):
+            nc.sync.dma_start(
+                out=y_dram[b].rearrange("(p t) n -> p (t n)", t=PACK), in_=res[:, b].rearrange("p t n -> p (t n)")
+            )

@@ -20,7 +20,10 @@ GROUPS = F // K_PASS
 BN_EPS = 1e-5
 RUN = 4
 
+COLS = 512
+
 SCALAR_COLS = 448
+LAST_SCALAR_COLS = 176
 
 FLOPS = 2 * (2 * F * C * BN)
 
@@ -39,39 +42,45 @@ def tile_nonlocallayer_pa_k_kernel(tc, inputs, Wv, bv, row, Wo, bo, gamma, beta,
 
     with ExitStack() as ctx:
         const = ctx.enter_context(tc.tile_pool(name="const", bufs=1))
-        raw = ctx.enter_context(tc.tile_pool(name="raw", bufs=GROUPS))
+        raw = ctx.enter_context(tc.tile_pool(name="raw", bufs=2 * GROUPS))
         work = ctx.enter_context(tc.tile_pool(name="work", bufs=2))
         psum_t = ctx.enter_context(tc.psum_pool(name="psum_t", bufs=2))
         psum_v = ctx.enter_context(tc.psum_pool(name="psum_v", bufs=2))
         psum_o = ctx.enter_context(tc.psum_pool(name="psum_o", bufs=1))
         ctx.enter_context(tc.manual_schedule())
 
-        def load_wv(g):
-            t = raw.tile([P, PACK, C], BF16, name="wv_raw")
+        def load_wv(g, u):
+            first = g * K_PASS + u * 2 * P
+            t = raw.tile([P, 2, C], BF16, name="wv_raw")
             nc.sync.dma_start(
-                out=t[:].rearrange("r (u e) c -> r u (e c)", e=2),
-                in_=Wv[g * K_PASS : (g + 1) * K_PASS, :].rearrange("(u r e) c -> r u (e c)", u=2, e=2),
+                out=t[:].rearrange("r e c -> r (e c)"),
+                in_=Wv[first : first + 2 * P, :].rearrange("(r e) c -> r (e c)", e=2),
             )
             return t
 
-        def load_wo(g):
-            t = raw.tile([P, PACK, K_PASS], BF16, name="wo_raw")
+        def load_wo(g, j):
+            t = raw.tile([P, 2, K_PASS], BF16, name="wo_raw")
             nc.sync.dma_start(
-                out=t[:], in_=Wo[:, g * K_PASS : (g + 1) * K_PASS].rearrange("(r t) f -> r t f", t=PACK)
+                out=t[:],
+                in_=Wo[:, g * K_PASS : (g + 1) * K_PASS].rearrange("(r t) f -> r t f", t=PACK)[:, 2 * j : 2 * j + 2, :],
             )
             return t
 
-        wv_raw = [load_wv(0)]
+        wv_raw = {(0, 0): load_wv(0, 0)}
         x_rows = const.tile([P, B, PACK, N], BF16)
         for b in range(B):
             nc.sync.dma_start(
                 out=x_rows[:, b].rearrange("p (h e) n -> p h (e n)", e=2),
                 in_=x_dram[b].rearrange("(h p e) n -> p h (e n)", h=2, e=2),
             )
-        wo_raw = [load_wo(0)]
-        for g in range(1, GROUPS):
-            wv_raw.append(load_wv(g))
-            wo_raw.append(load_wo(g))
+        wv_raw[(0, 1)] = load_wv(0, 1)
+        wo_raw = {}
+        for g in range(GROUPS):
+            for half in range(2):
+                if g + 1 < GROUPS:
+                    wv_raw[(g + 1, half)] = load_wv(g + 1, half)
+            for half in range(2):
+                wo_raw[(g, half)] = load_wo(g, half)
         x_res = const.tile([P, B, PACK, N], BF16)
         for b in range(B):
             nc.sync.dma_start(
@@ -99,29 +108,31 @@ def tile_nonlocallayer_pa_k_kernel(tc, inputs, Wv, bv, row, Wo, bo, gamma, beta,
         warm = const.tile([P, 1], F32)
         nc.scalar.activation(out=warm[:], in_=eps[:], func=ACT.Sqrt)
 
-        def transpose_weights(rows, name):
-            grouped = work.tile([P, PACK * P, 2], F32, name=name, align_bytes=64)
+        def transpose_half(rows, grouped, j):
+            bank = psum_t.tile([P, 2, 2 * P], F32, name="bank_t")
+            for i in range(2):
+                words = rows[:, i, :].bitcast(F32)
+                for h in range(2):
+                    nc.tensor.transpose(bank[:, h, i * P : (i + 1) * P], words[:, h * P : (h + 1) * P], ident[:])
+            nc.scalar.copy(out=grouped[:, 2 * j * P : 2 * (j + 1) * P, :], in_=bank[:].rearrange("p h c -> p c h"))
+
+        def transpose_group(halves, g, name):
+            grouped = work.tile([P, COLS, 2], F32, name=name, align_bytes=64)
             for j in range(2):
-                bank = psum_t.tile([P, 2, 2 * P], F32, name="bank_t")
-                for i in range(2):
-                    words = rows[:, 2 * j + i, :].bitcast(F32)
-                    for h in range(2):
-                        nc.tensor.transpose(
-                            bank[:, h, i * P : (i + 1) * P], words[:, h * P : (h + 1) * P], ident[:]
-                        )
-                nc.scalar.copy(
-                    out=grouped[:, 2 * j * P : 2 * (j + 1) * P, :], in_=bank[:].rearrange("p h c -> p c h")
-                )
+                transpose_half(halves[(g, j)], grouped, j)
             return grouped
 
-        def quantise(values, width, name, bufs):
-            words = work.tile([P, width], U32, name=name + "_words", bufs=bufs, align_bytes=64)
-            scales = work.tile([P, width], U8, name=name + "_scales", bufs=bufs, align_bytes=64)
-            nc.vector.quantize_mx(out=words[:].bitcast(FP8X4), scales=scales[:], in_=values)
+        def mx_operand(name, bufs):
+            words = work.tile([P, COLS], U32, name=name + "_words", bufs=bufs, align_bytes=64)
+            scales = work.tile([P, COLS], U8, name=name + "_scales", bufs=bufs, align_bytes=64)
             return words, scales
 
-        def quantise_weights(grouped, name, bufs):
-            return quantise(grouped[:].rearrange("p c h -> p (c h)").bitcast(BF16), PACK * P, name, bufs)
+        def quantise(values, operand, first, last):
+            words, scales = operand
+            nc.vector.quantize_mx(out=words[:, first:last].bitcast(FP8X4), scales=scales[:, first:last], in_=values)
+
+        def quantise_weights(grouped, operand, first, last):
+            quantise(grouped[:, first:last, :].rearrange("p c h -> p (c h)").bitcast(BF16), operand, first, last)
 
         def first_matmul(g, tiles):
             words, scales = wv_q[g]
@@ -132,8 +143,8 @@ def tile_nonlocallayer_pa_k_kernel(tc, inputs, Wv, bv, row, Wo, bo, gamma, beta,
                     out=bank[:],
                     lhsT=words[:, cols].bitcast(FP8X4),
                     lhsT_scale=scales[:, cols],
-                    rhs=x_words[:].bitcast(FP8X4),
-                    rhs_scale=x_scales[:],
+                    rhs=x_q[0][:].bitcast(FP8X4),
+                    rhs_scale=x_q[1][:],
                     start=True,
                     stop=True,
                 )
@@ -161,77 +172,99 @@ def tile_nonlocallayer_pa_k_kernel(tc, inputs, Wv, bv, row, Wo, bo, gamma, beta,
                     stop=(g == GROUPS - 1),
                 )
 
-        def relu_regroup_scalar(g, first, last):
+        def scalar_piece(g):
+            return (LAST_SCALAR_COLS if g == GROUPS - 1 else SCALAR_COLS) // 2
+
+        def relu_regroup_scalar(g, piece):
+            first = piece * scalar_piece(g)
+            last = first + scalar_piece(g)
             src, dst = side_by_side(gated[g][:, :, first:last], v1[g][:, first:last, :])
             nc.scalar.activation(out=dst, in_=src, func=ACT.Relu)
 
-        def relu_regroup_vector(g, first, last):
-            src, dst = side_by_side(gated[g][:, :, first:last], v1[g][:, first:last, :])
+        def relu_regroup_vector(g):
+            first = 2 * scalar_piece(g)
+            src, dst = side_by_side(gated[g][:, :, first:BN], v1[g][:, first:BN, :])
             nc.vector.tensor_scalar_max(out=dst, in0=src, scalar1=0.0)
 
         wv_q, wo_q, v1_q, gated, v1 = {}, {}, {}, {}, {}
         acc = [psum_o.tile([P, BN], F32, name="acc%d" % t) for t in range(PACK)]
 
-        wv_grouped = transpose_weights(wv_raw[0], "wv_grouped")
+        wv_grouped = work.tile([P, COLS, 2], F32, name="wv_grouped", align_bytes=64)
+        transpose_half(wv_raw[(0, 0)], wv_grouped, 0)
+
+        bv_bank = psum_v.tile([P, BN], F32, name="bank_v")
+        nc.tensor.transpose(bv_bank[:, 0:P], bv_rows[:].bitcast(F32), ident[:])
+        row_bank = psum_v.tile([P, BN], F32, name="bank_v")
+        nc.tensor.matmul(out=row_bank[:], lhsT=ones[:], rhs=row_one[:], start=True, stop=True)
+        row_all = const.tile([P, BN], F32)
+        nc.scalar.copy(out=row_all[:], in_=row_bank[:])
+
+        transpose_half(wv_raw[(0, 1)], wv_grouped, 1)
 
         x_grouped = const.tile([P, B, N, PACK], BF16, align_bytes=64)
         for b in range(B):
             src, dst = side_by_side(x_rows[:, b], x_grouped[:, b])
             nc.vector.tensor_copy(out=dst, in_=src)
-
-        bank = psum_v.tile([P, BN], F32, name="bank_v")
-        nc.tensor.transpose(bank[:, 0:P], bv_rows[:].bitcast(F32), ident[:])
+        x_q = mx_operand("x", 1)
+        quantise(x_grouped[:].rearrange("p b n t -> p (b n t)"), x_q, 0, COLS)
+        wv_q[0] = mx_operand("wv", 2)
+        quantise_weights(wv_grouped, wv_q[0], 0, COLS // 2)
         bv_f32 = const.tile([P, PACK * GROUPS], F32)
-        nc.vector.tensor_copy(out=bv_f32[:], in_=bank[:, 0 : 2 * GROUPS].bitcast(BF16))
+        nc.vector.tensor_copy(out=bv_f32[:], in_=bv_bank[:, 0 : 2 * GROUPS].bitcast(BF16))
+        quantise_weights(wv_grouped, wv_q[0], COLS // 2, COLS)
 
-        bank = psum_v.tile([P, BN], F32, name="bank_v")
-        nc.tensor.matmul(out=bank[:], lhsT=ones[:], rhs=row_one[:], start=True, stop=True)
-        row_all = const.tile([P, BN], F32)
-        nc.vector.tensor_copy(out=row_all[:], in_=bank[:])
-
-        x_words, x_scales = quantise(x_grouped[:].rearrange("p b n t -> p (b n t)"), BN, "x", 1)
-        wv_q[0] = quantise_weights(wv_grouped, "wv", 2)
-
-        half = SCALAR_COLS // 2
-        for i in range(GROUPS + 2):
-            if 0 <= i - 2:
-                v1_q[i - 2] = quantise(v1[i - 2][:].rearrange("p c t -> p (c t)"), BN, "v1", 2)
+        for i in range(GROUPS + 3):
+            if 0 <= i - 2 < GROUPS:
+                v1_q[i - 2] = mx_operand("v1", 2)
+                quantise(v1[i - 2][:].rearrange("p c t -> p (c t)"), v1_q[i - 2], 0, COLS)
             if i + 1 < GROUPS:
-                wv_grouped = transpose_weights(wv_raw[i + 1], "wv_grouped")
+                wv_grouped = transpose_group(wv_raw, i + 1, "wv_grouped")
             if i < GROUPS:
                 gated[i] = work.tile([P, PACK, BN], BF16, name="gated")
                 first_matmul(i, (0, 1))
-            if 0 <= i - 2:
-                second_matmul(i - 2, (0, 1))
+            if 0 <= i - 3:
+                second_matmul(i - 3, (2, 3))
             if i + 1 < GROUPS:
-                wv_q[i + 1] = quantise_weights(wv_grouped, "wv", 2)
+                wv_q[i + 1] = mx_operand("wv", 2)
+                quantise_weights(wv_grouped, wv_q[i + 1], 0, COLS)
             if 0 <= i - 1 < GROUPS:
                 v1[i - 1] = work.tile([P, BN, PACK], BF16, name="v1", align_bytes=64)
-                relu_regroup_scalar(i - 1, 0, half)
-                relu_regroup_vector(i - 1, SCALAR_COLS, BN)
+                relu_regroup_scalar(i - 1, 0)
+                relu_regroup_vector(i - 1)
             if i < GROUPS:
-                wo_grouped = transpose_weights(wo_raw[i], "wo_grouped")
+                wo_grouped = transpose_group(wo_raw, i, "wo_grouped")
                 first_matmul(i, (2, 3))
-            if 0 <= i - 2:
-                second_matmul(i - 2, (2, 3))
+            if 0 <= i - 2 < GROUPS:
+                second_matmul(i - 2, (0, 1))
             if i < GROUPS:
-                wo_q[i] = quantise_weights(wo_grouped, "wo", 3)
+                wo_q[i] = mx_operand("wo", 4)
+                quantise_weights(wo_grouped, wo_q[i], 0, COLS)
             if 0 <= i - 1 < GROUPS:
-                relu_regroup_scalar(i - 1, half, SCALAR_COLS)
+                relu_regroup_scalar(i - 1, 1)
 
         chan = const.tile([P, 3, PACK], F32)
         nc.vector.tensor_copy(out=chan[:], in_=chan_bf[:, :, 0:PACK])
         res = const.tile([P, B, PACK, N], F32)
         stats = const.tile([P, PACK, 6], F32)
         mean_var = const.tile([P, PACK, 2], F32)
+        positive = []
         for t in range(PACK):
-            positive = work.tile([P, B, N], F32, name="positive")
+            positive.append(work.tile([P, B, N], F32, name="positive", bufs=PACK))
             nc.scalar.activation(
-                out=positive[:].rearrange("p b n -> p (b n)"), in_=acc[t][:], func=ACT.Relu, bias=chan[:, 0, t : t + 1]
+                out=positive[t][:].rearrange("p b n -> p (b n)"), in_=acc[t][:], func=ACT.Relu, bias=chan[:, 0, t : t + 1]
             )
-            nc.vector.tensor_tensor(out=res[:, :, t, :], in0=positive[:], in1=x_res[:, :, t, :], op=ALU.add)
+
+        def statistics(t):
             nc.vector.bn_stats(out=stats[:, t, :], in_=res[:, :, t, :])
             nc.vector.bn_aggr(out=mean_var[:, t, :], in_=stats[:, t, :])
+
+        for t in (1, 3):
+            nc.gpsimd.tensor_tensor(out=res[:, :, t, :], in0=positive[t][:], in1=x_res[:, :, t, :], op=ALU.add)
+        for t in (0, 2):
+            nc.vector.tensor_tensor(out=res[:, :, t, :], in0=positive[t][:], in1=x_res[:, :, t, :], op=ALU.add)
+            statistics(t)
+        for t in (1, 3):
+            statistics(t)
         gain = const.tile([P, PACK], F32)
         shift = const.tile([P, PACK], F32)
         nc.scalar.activation(out=gain[:], in_=mean_var[:, :, 1], func=ACT.Sqrt, bias=eps[:, 0:1])
@@ -240,24 +273,12 @@ def tile_nonlocallayer_pa_k_kernel(tc, inputs, Wv, bv, row, Wo, bo, gamma, beta,
         nc.vector.tensor_tensor(out=shift[:], in0=mean_var[:, :, 0], in1=gain[:], op=ALU.mult)
         nc.vector.tensor_tensor(out=shift[:], in0=chan[:, 2, :], in1=shift[:], op=ALU.subtract)
         for t in range(PACK):
-            if t % 2 == 0:
-                nc.vector.tensor_scalar(
-                    out=res[:, :, t, :],
-                    in0=res[:, :, t, :],
-                    scalar1=gain[:, t : t + 1],
-                    scalar2=shift[:, t : t + 1],
-                    op0=ALU.mult,
-                    op1=ALU.add,
-                )
-            else:
-                nc.scalar.activation(
-                    out=res[:, :, t, :],
-                    in_=res[:, :, t, :],
-                    func=ACT.Identity,
-                    scale=gain[:, t : t + 1],
-                    bias=shift[:, t : t + 1],
-                )
-        for b in range(B):
-            nc.sync.dma_start(
-                out=y_dram[b].rearrange("(p t) n -> p (t n)", t=PACK), in_=res[:, b].rearrange("p t n -> p (t n)")
+            nc.vector.tensor_scalar(
+                out=res[:, :, t, :],
+                in0=res[:, :, t, :],
+                scalar1=gain[:, t : t + 1],
+                scalar2=shift[:, t : t + 1],
+                op0=ALU.mult,
+                op1=ALU.add,
             )
+            nc.sync.dma_start(out=y_dram.rearrange("b (p t) n -> t p b n", t=PACK)[t], in_=res[:, :, t, :])

@@ -22,8 +22,9 @@ RUN = 4
 
 COLS = 512
 
-SCALAR_COLS = 448
+SCALAR_COLS = 384
 LAST_SCALAR_COLS = 176
+BF16_TOP = 3.4e38
 
 FLOPS = 2 * (2 * F * C * BN)
 
@@ -181,10 +182,15 @@ def tile_nonlocallayer_pa_k_kernel(tc, inputs, Wv, bv, row, Wo, bo, gamma, beta,
             src, dst = side_by_side(gated[g][:, :, first:last], v1[g][:, first:last, :])
             nc.scalar.activation(out=dst, in_=src, func=ACT.Relu)
 
-        def relu_regroup_vector(g):
+        def relu_regroup_rest(g):
             first = 2 * scalar_piece(g)
             src, dst = side_by_side(gated[g][:, :, first:BN], v1[g][:, first:BN, :])
-            nc.vector.tensor_scalar_max(out=dst, in0=src, scalar1=0.0)
+            if g == GROUPS - 1:
+                nc.vector.tensor_scalar_max(out=dst, in0=src, scalar1=0.0)
+            else:
+                nc.gpsimd.tensor_scalar(
+                    out=dst, in0=src, scalar1=BF16_TOP, scalar2=0.0, op0=ALU.min, op1=ALU.max
+                )
 
         wv_q, wo_q, v1_q, gated, v1 = {}, {}, {}, {}, {}
         acc = [psum_o.tile([P, BN], F32, name="acc%d" % t) for t in range(PACK)]
@@ -230,7 +236,7 @@ def tile_nonlocallayer_pa_k_kernel(tc, inputs, Wv, bv, row, Wo, bo, gamma, beta,
             if 0 <= i - 1 < GROUPS:
                 v1[i - 1] = work.tile([P, BN, PACK], BF16, name="v1", align_bytes=64)
                 relu_regroup_scalar(i - 1, 0)
-                relu_regroup_vector(i - 1)
+                relu_regroup_rest(i - 1)
             if i < GROUPS:
                 wo_grouped = transpose_group(wo_raw, i, "wo_grouped")
                 first_matmul(i, (2, 3))

@@ -23,7 +23,7 @@ RUN = 4
 COLS = 512
 
 SCALAR_COLS = 384
-LAST_SCALAR_COLS = 176
+LAST_VECTOR_COLS = 128
 BF16_TOP = 3.4e38
 
 FLOPS = 2 * (2 * F * C * BN)
@@ -67,13 +67,18 @@ def tile_nonlocallayer_pa_k_kernel(tc, inputs, Wv, bv, row, Wo, bo, gamma, beta,
             )
             return t
 
-        wv_raw = {(0, 0): load_wv(0, 0)}
         x_rows = const.tile([P, B, PACK, N], BF16)
-        for b in range(B):
+
+        def load_x(b):
             nc.sync.dma_start(
                 out=x_rows[:, b].rearrange("p (h e) n -> p h (e n)", e=2),
                 in_=x_dram[b].rearrange("(h p e) n -> p h (e n)", h=2, e=2),
             )
+
+        wv_raw = {}
+        load_x(0)
+        wv_raw[(0, 0)] = load_wv(0, 0)
+        load_x(1)
         wv_raw[(0, 1)] = load_wv(0, 1)
         wo_raw = {}
         for g in range(GROUPS):
@@ -99,15 +104,16 @@ def tile_nonlocallayer_pa_k_kernel(tc, inputs, Wv, bv, row, Wo, bo, gamma, beta,
         masks.make_identity(nc, ident[:])
 
         bv_rows = const.tile([P, 2 * P], BF16)
-        nc.vector.memset(bv_rows[:], 0.0)
         nc.scalar.dma_start(out=bv_rows[0 : 2 * GROUPS, :], in_=bv.rearrange("(j w) -> j w", w=2 * P))
-        row_one = const.tile([P, BN], BF16)
-        nc.vector.memset(row_one[:], 0.0)
-        nc.scalar.dma_start(out=row_one[0:1, :], in_=row.rearrange("b n -> (b n)").unsqueeze(0))
-        ones = const.tile([P, P], BF16)
-        nc.vector.memset(ones[:], 1.0)
+        row_few = const.tile([P, BN], BF16)
+        nc.scalar.dma_start(out=row_few[0:32, :], in_=row.rearrange("b n -> (b n)").partition_broadcast(32))
+        share = const.tile([P, P], BF16)
+        nc.vector.memset(share[:], 1.0 / 32)
+        for lo, hi in ((32, 64), (64, P)):
+            nc.vector.memset(bv_rows[lo:hi, :], 0.0)
+            nc.vector.memset(row_few[lo:hi, :], 0.0)
         warm = const.tile([P, 1], F32)
-        nc.scalar.activation(out=warm[:], in_=eps[:], func=ACT.Sqrt)
+        nc.scalar.activation(out=warm[:], in_=eps[:], func=ACT.Abs_reciprocal_sqrt)
 
         def transpose_half(rows, grouped, j):
             bank = psum_t.tile([P, 2, 2 * P], F32, name="bank_t")
@@ -132,159 +138,311 @@ def tile_nonlocallayer_pa_k_kernel(tc, inputs, Wv, bv, row, Wo, bo, gamma, beta,
             words, scales = operand
             nc.vector.quantize_mx(out=words[:, first:last].bitcast(FP8X4), scales=scales[:, first:last], in_=values)
 
+        def new_gated(g):
+            gated[g] = work.tile([P, PACK, BN], BF16, name="gated")
+
+        def new_v1(g):
+            v1[g] = work.tile([P, BN, PACK], BF16, name="v1", align_bytes=64)
+
         def quantise_weights(grouped, operand, first, last):
             quantise(grouped[:, first:last, :].rearrange("p c h -> p (c h)").bitcast(BF16), operand, first, last)
 
-        def first_matmul(g, tiles):
+        def first_matmul(g, t, bank):
             words, scales = wv_q[g]
-            for t in tiles:
-                cols = slice(t * P, (t + 1) * P)
-                bank = psum_v.tile([P, BN], F32, name="bank_v")
-                nc.tensor.matmul_mx(
-                    out=bank[:],
-                    lhsT=words[:, cols].bitcast(FP8X4),
-                    lhsT_scale=scales[:, cols],
-                    rhs=x_q[0][:].bitcast(FP8X4),
-                    rhs_scale=x_q[1][:],
-                    start=True,
-                    stop=True,
-                )
-                nc.vector.scalar_tensor_tensor(
-                    out=gated[g][:, t, :],
-                    in0=bank[:],
-                    scalar=bv_f32[:, PACK * g + t : PACK * g + t + 1],
-                    in1=row_all[:],
-                    op0=ALU.add,
-                    op1=ALU.mult,
-                )
+            cols = slice(t * P, (t + 1) * P)
+            nc.tensor.matmul_mx(
+                out=bank,
+                lhsT=words[:, cols].bitcast(FP8X4),
+                lhsT_scale=scales[:, cols],
+                rhs=x_q[0][:].bitcast(FP8X4),
+                rhs_scale=x_q[1][:],
+                start=True,
+                stop=True,
+            )
 
-        def second_matmul(g, tiles):
+        def gate(g, t, bank, first, last):
+            nc.vector.scalar_tensor_tensor(
+                out=gated[g][:, t, first:last],
+                in0=bank[:, first:last],
+                scalar=bv_f32[:, PACK * g + t : PACK * g + t + 1],
+                in1=row_all[:, first:last],
+                op0=ALU.add,
+                op1=ALU.mult,
+            )
+
+        def gated_tiles(g, tiles):
+            for t in tiles:
+                bank = psum_v.tile([P, BN], F32, name="bank_v")
+                first_matmul(g, t, bank[:])
+                gate(g, t, bank, 0, BN)
+
+        def second_matmul(g, tiles, first=0, last=BN):
             w_words, w_scales = wo_q[g]
             v_words, v_scales = v1_q[g]
             for t in tiles:
                 cols = slice(t * P, (t + 1) * P)
                 nc.tensor.matmul_mx(
-                    out=acc[t][:],
+                    out=acc[t][:, first:last],
                     lhsT=w_words[:, cols].bitcast(FP8X4),
                     lhsT_scale=w_scales[:, cols],
-                    rhs=v_words[:].bitcast(FP8X4),
-                    rhs_scale=v_scales[:],
+                    rhs=v_words[:, first:last].bitcast(FP8X4),
+                    rhs_scale=v_scales[:, first:last],
                     start=(g == 0),
-                    stop=(g == GROUPS - 1),
+                    stop=(g == GROUPS - 1 and last == BN),
                 )
 
-        def scalar_piece(g):
-            return (LAST_SCALAR_COLS if g == GROUPS - 1 else SCALAR_COLS) // 2
-
-        def relu_regroup_scalar(g, piece):
-            first = piece * scalar_piece(g)
-            last = first + scalar_piece(g)
+        def regroup_scalar(g, first, last):
             src, dst = side_by_side(gated[g][:, :, first:last], v1[g][:, first:last, :])
             nc.scalar.activation(out=dst, in_=src, func=ACT.Relu)
 
-        def relu_regroup_rest(g):
-            first = 2 * scalar_piece(g)
-            src, dst = side_by_side(gated[g][:, :, first:BN], v1[g][:, first:BN, :])
-            if g == GROUPS - 1:
-                nc.vector.tensor_scalar_max(out=dst, in0=src, scalar1=0.0)
-            else:
-                nc.gpsimd.tensor_scalar(
-                    out=dst, in0=src, scalar1=BF16_TOP, scalar2=0.0, op0=ALU.min, op1=ALU.max
-                )
+        def regroup_gpsimd(g, first, last):
+            src, dst = side_by_side(gated[g][:, :, first:last], v1[g][:, first:last, :])
+            nc.gpsimd.tensor_scalar(out=dst, in0=src, scalar1=BF16_TOP, scalar2=0.0, op0=ALU.min, op1=ALU.max)
+
+        def regroup_vector(g, first, last):
+            src, dst = side_by_side(gated[g][:, :, first:last], v1[g][:, first:last, :])
+            nc.vector.tensor_scalar_max(out=dst, in0=src, scalar1=0.0)
+
+        def quantise_v1(g, first, last):
+            quantise(v1[g][:, first:last, :].rearrange("p c t -> p (c t)"), v1_q[g], first, last)
 
         wv_q, wo_q, v1_q, gated, v1 = {}, {}, {}, {}, {}
         acc = [psum_o.tile([P, BN], F32, name="acc%d" % t) for t in range(PACK)]
 
-        wv_grouped = work.tile([P, COLS, 2], F32, name="wv_grouped", align_bytes=64)
-        transpose_half(wv_raw[(0, 0)], wv_grouped, 0)
-
         bv_bank = psum_v.tile([P, BN], F32, name="bank_v")
         nc.tensor.transpose(bv_bank[:, 0:P], bv_rows[:].bitcast(F32), ident[:])
-        row_bank = psum_v.tile([P, BN], F32, name="bank_v")
-        nc.tensor.matmul(out=row_bank[:], lhsT=ones[:], rhs=row_one[:], start=True, stop=True)
-        row_all = const.tile([P, BN], F32)
-        nc.scalar.copy(out=row_all[:], in_=row_bank[:])
+        bv_f32 = const.tile([P, PACK * GROUPS], F32)
 
-        transpose_half(wv_raw[(0, 1)], wv_grouped, 1)
-
+        wv_grouped = work.tile([P, COLS, 2], F32, name="wv_grouped", align_bytes=64)
         x_grouped = const.tile([P, B, N, PACK], BF16, align_bytes=64)
-        for b in range(B):
+        x_q = mx_operand("x", 1)
+        wv_q[0] = mx_operand("wv", 2)
+
+        def regroup_x(b):
             src, dst = side_by_side(x_rows[:, b], x_grouped[:, b])
             nc.vector.tensor_copy(out=dst, in_=src)
-        x_q = mx_operand("x", 1)
-        quantise(x_grouped[:].rearrange("p b n t -> p (b n t)"), x_q, 0, COLS)
-        wv_q[0] = mx_operand("wv", 2)
-        quantise_weights(wv_grouped, wv_q[0], 0, COLS // 2)
-        bv_f32 = const.tile([P, PACK * GROUPS], F32)
-        nc.vector.tensor_copy(out=bv_f32[:], in_=bv_bank[:, 0 : 2 * GROUPS].bitcast(BF16))
-        quantise_weights(wv_grouped, wv_q[0], COLS // 2, COLS)
 
-        for i in range(GROUPS + 3):
-            if 0 <= i - 2 < GROUPS:
-                v1_q[i - 2] = mx_operand("v1", 2)
-                quantise(v1[i - 2][:].rearrange("p c t -> p (c t)"), v1_q[i - 2], 0, COLS)
-            if i + 1 < GROUPS:
-                wv_grouped = transpose_group(wv_raw, i + 1, "wv_grouped")
-            if i < GROUPS:
-                gated[i] = work.tile([P, PACK, BN], BF16, name="gated")
-                first_matmul(i, (0, 1))
-            if 0 <= i - 3:
-                second_matmul(i - 3, (2, 3))
-            if i + 1 < GROUPS:
-                wv_q[i + 1] = mx_operand("wv", 2)
-                quantise_weights(wv_grouped, wv_q[i + 1], 0, COLS)
-            if 0 <= i - 1 < GROUPS:
-                v1[i - 1] = work.tile([P, BN, PACK], BF16, name="v1", align_bytes=64)
-                relu_regroup_scalar(i - 1, 0)
-                relu_regroup_rest(i - 1)
-            if i < GROUPS:
-                wo_grouped = transpose_group(wo_raw, i, "wo_grouped")
-                first_matmul(i, (2, 3))
-            if 0 <= i - 2 < GROUPS:
-                second_matmul(i - 2, (0, 1))
-            if i < GROUPS:
-                wo_q[i] = mx_operand("wo", 4)
-                quantise_weights(wo_grouped, wo_q[i], 0, COLS)
-            if 0 <= i - 1 < GROUPS:
-                relu_regroup_scalar(i - 1, 1)
+        def quantise_x(b):
+            quantise(x_grouped[:, b].rearrange("p n t -> p (n t)"), x_q, b * N, (b + 1) * N)
+
+        regroup_x(0)
+        nc.vector.tensor_copy(out=bv_f32[:], in_=bv_bank[:, 0 : 2 * GROUPS].bitcast(BF16))
+        quantise_x(0)
+        transpose_half(wv_raw[(0, 0)], wv_grouped, 0)
+        row_bank = psum_v.tile([P, BN], F32, name="bank_v")
+        nc.tensor.matmul(out=row_bank[:], lhsT=share[:], rhs=row_few[:], start=True, stop=True)
+        transpose_half(wv_raw[(0, 1)], wv_grouped, 1)
+        row_all = const.tile([P, BN], F32)
+        regroup_x(1)
+        quantise_weights(wv_grouped, wv_q[0], 0, COLS // 2)
+        quantise_x(1)
+        nc.vector.tensor_copy(out=row_all[:], in_=row_bank[:])
 
         chan = const.tile([P, 3, PACK], F32)
-        nc.vector.tensor_copy(out=chan[:], in_=chan_bf[:, :, 0:PACK])
-        res = const.tile([P, B, PACK, N], F32)
-        stats = const.tile([P, PACK, 6], F32)
-        mean_var = const.tile([P, PACK, 2], F32)
-        positive = []
-        for t in range(PACK):
-            positive.append(work.tile([P, B, N], F32, name="positive", bufs=PACK))
-            nc.scalar.activation(
-                out=positive[t][:].rearrange("p b n -> p (b n)"), in_=acc[t][:], func=ACT.Relu, bias=chan[:, 0, t : t + 1]
+        neg_bo = const.tile([P, PACK], F32)
+        x_bo = const.tile([P, PACK - 1, BN], F32)
+
+        def prepare_channels():
+            nc.gpsimd.tensor_copy(out=chan[:], in_=chan_bf[:, :, 0:PACK])
+            nc.gpsimd.tensor_scalar(
+                out=neg_bo[:], in0=chan[:, 0, :], scalar1=-1.0, scalar2=0.0, op0=ALU.mult, op1=ALU.add
             )
 
-        def statistics(t):
-            nc.vector.bn_stats(out=stats[:, t, :], in_=res[:, :, t, :])
-            nc.vector.bn_aggr(out=mean_var[:, t, :], in_=stats[:, t, :])
-
-        for t in (1, 3):
-            nc.gpsimd.tensor_tensor(out=res[:, :, t, :], in0=positive[t][:], in1=x_res[:, :, t, :], op=ALU.add)
-        for t in (0, 2):
-            nc.vector.tensor_tensor(out=res[:, :, t, :], in0=positive[t][:], in1=x_res[:, :, t, :], op=ALU.add)
-            statistics(t)
-        for t in (1, 3):
-            statistics(t)
-        gain = const.tile([P, PACK], F32)
-        shift = const.tile([P, PACK], F32)
-        nc.scalar.activation(out=gain[:], in_=mean_var[:, :, 1], func=ACT.Sqrt, bias=eps[:, 0:1])
-        nc.vector.reciprocal(out=gain[:], in_=gain[:])
-        nc.vector.tensor_tensor(out=gain[:], in0=gain[:], in1=chan[:, 1, :], op=ALU.mult)
-        nc.vector.tensor_tensor(out=shift[:], in0=mean_var[:, :, 0], in1=gain[:], op=ALU.mult)
-        nc.vector.tensor_tensor(out=shift[:], in0=chan[:, 2, :], in1=shift[:], op=ALU.subtract)
-        for t in range(PACK):
-            nc.vector.tensor_scalar(
-                out=res[:, :, t, :],
-                in0=res[:, :, t, :],
-                scalar1=gain[:, t : t + 1],
-                scalar2=shift[:, t : t + 1],
+        def prepare_x(t):
+            nc.gpsimd.tensor_scalar(
+                out=x_bo[:, t, :].rearrange("p (b n) -> p b n", b=B),
+                in0=x_res[:, :, t, :],
+                scalar1=1.0,
+                scalar2=chan[:, 0, t : t + 1],
                 op0=ALU.mult,
                 op1=ALU.add,
             )
-            nc.sync.dma_start(out=y_dram.rearrange("b (p t) n -> t p b n", t=PACK)[t], in_=res[:, :, t, :])
+
+        LAST = GROUPS - 1
+        for i in range(LAST):
+            if 0 <= i - 2:
+                v1_q[i - 2] = mx_operand("v1", 2)
+                quantise_v1(i - 2, 0, BN)
+            new_gated(i)
+            if i == 0:
+                wv_grouped_0 = wv_grouped
+                wv_grouped = work.tile([P, COLS, 2], F32, name="wv_grouped", align_bytes=64)
+                transpose_half(wv_raw[(1, 0)], wv_grouped, 0)
+                gated_tiles(0, (0, 1))
+                quantise_weights(wv_grouped_0, wv_q[0], COLS // 2, COLS)
+                transpose_half(wv_raw[(1, 1)], wv_grouped, 1)
+                gated_tiles(0, (2, 3))
+            else:
+                wv_grouped = transpose_group(wv_raw, i + 1, "wv_grouped")
+                gated_tiles(i, (0, 1))
+            if 0 <= i - 3:
+                second_matmul(i - 3, (2, 3))
+            wv_q[i + 1] = mx_operand("wv", 2)
+            quantise_weights(wv_grouped, wv_q[i + 1], 0, COLS)
+            if 0 <= i - 1:
+                new_v1(i - 1)
+                regroup_scalar(i - 1, 0, SCALAR_COLS // 2)
+                regroup_gpsimd(i - 1, SCALAR_COLS, BN)
+            if i == LAST - 4:
+                prepare_channels()
+            if LAST - 3 <= i:
+                prepare_x(i - (LAST - 3))
+            wo_grouped = transpose_group(wo_raw, i, "wo_grouped")
+            if i > 0:
+                gated_tiles(i, (2, 3))
+            if 0 <= i - 2:
+                second_matmul(i - 2, (0, 1))
+            wo_q[i] = mx_operand("wo", 4)
+            quantise_weights(wo_grouped, wo_q[i], 0, COLS)
+            if 0 <= i - 1:
+                regroup_scalar(i - 1, SCALAR_COLS // 2, SCALAR_COLS)
+
+        HALF = BN // 2
+        v1_q[LAST - 2] = mx_operand("v1", 2)
+        quantise_v1(LAST - 2, 0, BN)
+        wo_grouped = transpose_group(wo_raw, LAST, "wo_grouped")
+        new_gated(LAST)
+        banks = []
+        for t in range(2):
+            banks.append(psum_v.tile([P, BN], F32, name="bank_v")[:])
+            first_matmul(LAST, t, banks[t])
+            gate(LAST, t, banks[t], 0, HALF)
+        second_matmul(LAST - 3, (2, 3))
+        wo_q[LAST] = mx_operand("wo", 4)
+        quantise_weights(wo_grouped, wo_q[LAST], 0, COLS)
+        new_v1(LAST - 1)
+        regroup_scalar(LAST - 1, 0, SCALAR_COLS)
+        regroup_gpsimd(LAST - 1, SCALAR_COLS, BN)
+        for t in range(2, PACK):
+            banks.append(psum_t.tile([P, 2, 2 * P], F32, name="bank_t")[:].rearrange("p h c -> p (h c)"))
+            first_matmul(LAST, t, banks[t])
+            gate(LAST, t, banks[t], 0, HALF)
+        second_matmul(LAST - 2, range(PACK))
+        new_v1(LAST)
+        regroup_scalar(LAST, 0, HALF)
+        v1_q[LAST - 1] = mx_operand("v1", 2)
+        quantise_v1(LAST - 1, 0, BN)
+        second_matmul(LAST - 1, range(PACK))
+        for t in range(PACK):
+            gate(LAST, t, banks[t], HALF, BN)
+        v1_q[LAST] = mx_operand("v1", 2)
+        quantise_v1(LAST, 0, HALF)
+        second_matmul(LAST, range(PACK), 0, HALF)
+        regroup_scalar(LAST, HALF, BN - LAST_VECTOR_COLS)
+        regroup_vector(LAST, BN - LAST_VECTOR_COLS, BN)
+        quantise_v1(LAST, HALF, BN)
+        second_matmul(LAST, range(PACK), HALF, BN)
+
+        res = const.tile([P, PACK, BN], F32)
+        total = const.tile([P, PACK], F32)
+        neg_mean = const.tile([P, PACK], F32)
+        square = const.tile([P, BN], F32)
+        sum_square = const.tile([P, PACK], F32)
+        rstd = const.tile([P, PACK], F32)
+        stats = const.tile([P, 6], F32)
+        mean_var = const.tile([P, 2], F32)
+        gain = const.tile([P, PACK], F32)
+        shift = const.tile([P, PACK], F32)
+
+        def col(tile, t):
+            return tile[:, t : t + 1]
+
+        def residual(t):
+            nc.vector.scalar_tensor_tensor(
+                out=res[:, t, :],
+                in0=acc[t][:],
+                scalar=col(neg_bo, t),
+                in1=x_bo[:, t, :],
+                op0=ALU.max,
+                op1=ALU.add,
+                accum_out=col(total, t),
+            )
+
+        def negative_mean(t):
+            nc.vector.tensor_scalar(
+                out=col(neg_mean, t), in0=col(total, t), scalar1=-1.0 / BN, scalar2=None, op0=ALU.mult
+            )
+
+        def squared_deviations(t):
+            nc.scalar.activation(
+                out=square[:], in_=res[:, t, :], func=ACT.Square, bias=col(neg_mean, t), accum_out=col(sum_square, t)
+            )
+
+        def reciprocal_deviation(t, variance, scale):
+            nc.scalar.activation(
+                out=col(rstd, t), in_=variance, func=ACT.Abs_reciprocal_sqrt, scale=scale, bias=eps[:, 0:1]
+            )
+
+        def make_gain(t):
+            nc.vector.tensor_tensor(out=col(gain, t), in0=col(rstd, t), in1=chan[:, 1, t : t + 1], op=ALU.mult)
+
+        def make_shift(t):
+            nc.vector.tensor_scalar(
+                out=col(shift, t),
+                in0=col(neg_mean, t),
+                scalar1=col(gain, t),
+                scalar2=chan[:, 2, t : t + 1],
+                op0=ALU.mult,
+                op1=ALU.add,
+            )
+
+        def norm_vector(t):
+            nc.vector.tensor_scalar(
+                out=res[:, t, :],
+                in0=res[:, t, :],
+                scalar1=col(gain, t),
+                scalar2=col(shift, t),
+                op0=ALU.mult,
+                op1=ALU.add,
+            )
+
+        def norm_scalar(t):
+            nc.scalar.activation(
+                out=res[:, t, :], in_=res[:, t, :], func=ACT.Identity, scale=col(gain, t), bias=col(shift, t)
+            )
+
+        def store(t):
+            nc.sync.dma_start(
+                out=y_dram.rearrange("b (p t) n -> t p b n", t=PACK)[t],
+                in_=res[:, t, :].rearrange("p (b n) -> p b n", b=B),
+            )
+
+        positive = const.tile([P, B, N], F32)
+        nc.scalar.activation(
+            out=positive[:].rearrange("p b n -> p (b n)"), in_=acc[3][:], func=ACT.Relu, bias=chan[:, 0, 3:4]
+        )
+        residual(0)
+        nc.gpsimd.tensor_tensor(
+            out=res[:, 3, :].rearrange("p (b n) -> p b n", b=B), in0=positive[:], in1=x_res[:, :, 3, :], op=ALU.add
+        )
+        residual(1)
+        negative_mean(0)
+        squared_deviations(0)
+        reciprocal_deviation(0, col(sum_square, 0), 1.0 / BN)
+        residual(2)
+        negative_mean(1)
+        squared_deviations(1)
+        reciprocal_deviation(1, col(sum_square, 1), 1.0 / BN)
+        make_gain(0)
+        negative_mean(2)
+        nc.vector.bn_stats(out=stats[:], in_=res[:, 3, :])
+        make_shift(0)
+        nc.vector.bn_aggr(out=mean_var[:], in_=stats[:])
+        norm_vector(0)
+        store(0)
+        reciprocal_deviation(3, mean_var[:, 1:2], 1.0)
+        squared_deviations(2)
+        reciprocal_deviation(2, col(sum_square, 2), 1.0 / BN)
+        make_gain(1)
+        nc.vector.tensor_scalar(out=col(neg_mean, 3), in0=mean_var[:, 0:1], scalar1=-1.0, scalar2=None, op0=ALU.mult)
+        make_shift(1)
+        make_gain(3)
+        norm_vector(1)
+        store(1)
+        make_shift(3)
+        make_gain(2)
+        norm_vector(3)
+        store(3)
+        make_shift(2)
+        norm_scalar(2)
+        store(2)

@@ -22,8 +22,11 @@ RUN = 4
 
 COLS = 512
 
+RAW_HALVES = 16
+
 SCALAR_COLS = 384
-LAST_VECTOR_COLS = 128
+LAST_VECTOR_COLS = 160
+DEFERRED = 8
 BF16_TOP = 3.4e38
 
 FLOPS = 2 * (2 * F * C * BN)
@@ -43,9 +46,9 @@ def tile_nonlocallayer_pa_k_kernel(tc, inputs, Wv, bv, row, Wo, bo, gamma, beta,
 
     with ExitStack() as ctx:
         const = ctx.enter_context(tc.tile_pool(name="const", bufs=1))
-        raw = ctx.enter_context(tc.tile_pool(name="raw", bufs=2 * GROUPS))
+        raw = ctx.enter_context(tc.tile_pool(name="raw", bufs=RAW_HALVES))
         work = ctx.enter_context(tc.tile_pool(name="work", bufs=2))
-        psum_t = ctx.enter_context(tc.psum_pool(name="psum_t", bufs=2))
+        psum_t = ctx.enter_context(tc.psum_pool(name="psum_t", bufs=3))
         psum_v = ctx.enter_context(tc.psum_pool(name="psum_v", bufs=2))
         psum_o = ctx.enter_context(tc.psum_pool(name="psum_o", bufs=1))
         ctx.enter_context(tc.manual_schedule())
@@ -207,7 +210,10 @@ def tile_nonlocallayer_pa_k_kernel(tc, inputs, Wv, bv, row, Wo, bo, gamma, beta,
             quantise(v1[g][:, first:last, :].rearrange("p c t -> p (c t)"), v1_q[g], first, last)
 
         wv_q, wo_q, v1_q, gated, v1 = {}, {}, {}, {}, {}
-        acc = [psum_o.tile([P, BN], F32, name="acc%d" % t) for t in range(PACK)]
+        acc = []
+        for t in range(PACK - 1):
+            bank = psum_o.tile([P, BN], F32, name="acc%d" % t)
+            acc.append(bank[:])
 
         bv_bank = psum_v.tile([P, BN], F32, name="bank_v")
         nc.tensor.transpose(bv_bank[:, 0:P], bv_rows[:].bitcast(F32), ident[:])
@@ -240,7 +246,7 @@ def tile_nonlocallayer_pa_k_kernel(tc, inputs, Wv, bv, row, Wo, bo, gamma, beta,
 
         chan = const.tile([P, 3, PACK], F32)
         neg_bo = const.tile([P, PACK], F32)
-        x_bo = const.tile([P, PACK - 1, BN], F32)
+        x_bo = const.tile([P, PACK, BN], F32)
 
         def prepare_channels():
             nc.gpsimd.tensor_copy(out=chan[:], in_=chan_bf[:, :, 0:PACK])
@@ -261,7 +267,7 @@ def tile_nonlocallayer_pa_k_kernel(tc, inputs, Wv, bv, row, Wo, bo, gamma, beta,
         LAST = GROUPS - 1
         for i in range(LAST):
             if 0 <= i - 2:
-                v1_q[i - 2] = mx_operand("v1", 2)
+                v1_q[i - 2] = mx_operand("v1", GROUPS)
                 quantise_v1(i - 2, 0, BN)
             new_gated(i)
             if i == 0:
@@ -276,62 +282,73 @@ def tile_nonlocallayer_pa_k_kernel(tc, inputs, Wv, bv, row, Wo, bo, gamma, beta,
                 wv_grouped = transpose_group(wv_raw, i + 1, "wv_grouped")
                 gated_tiles(i, (0, 1))
             if 0 <= i - 3:
-                second_matmul(i - 3, (2, 3))
+                second_matmul(i - 3, (2,))
             wv_q[i + 1] = mx_operand("wv", 2)
             quantise_weights(wv_grouped, wv_q[i + 1], 0, COLS)
             if 0 <= i - 1:
                 new_v1(i - 1)
                 regroup_scalar(i - 1, 0, SCALAR_COLS // 2)
                 regroup_gpsimd(i - 1, SCALAR_COLS, BN)
-            if i == LAST - 4:
+            if i == LAST - 5:
                 prepare_channels()
-            if LAST - 3 <= i:
-                prepare_x(i - (LAST - 3))
+            if LAST - 4 <= i:
+                prepare_x(i - (LAST - 4))
             wo_grouped = transpose_group(wo_raw, i, "wo_grouped")
             if i > 0:
                 gated_tiles(i, (2, 3))
             if 0 <= i - 2:
                 second_matmul(i - 2, (0, 1))
-            wo_q[i] = mx_operand("wo", 4)
+            wo_q[i] = mx_operand("wo", GROUPS)
             quantise_weights(wo_grouped, wo_q[i], 0, COLS)
             if 0 <= i - 1:
                 regroup_scalar(i - 1, SCALAR_COLS // 2, SCALAR_COLS)
 
         HALF = BN // 2
-        v1_q[LAST - 2] = mx_operand("v1", 2)
+        v1_q[LAST - 2] = mx_operand("v1", GROUPS)
         quantise_v1(LAST - 2, 0, BN)
         wo_grouped = transpose_group(wo_raw, LAST, "wo_grouped")
         new_gated(LAST)
         banks = []
         for t in range(2):
-            banks.append(psum_v.tile([P, BN], F32, name="bank_v")[:])
+            bank = psum_v.tile([P, BN], F32, name="bank_v")
+            banks.append(bank[:])
             first_matmul(LAST, t, banks[t])
             gate(LAST, t, banks[t], 0, HALF)
-        second_matmul(LAST - 3, (2, 3))
-        wo_q[LAST] = mx_operand("wo", 4)
+        wo_q[LAST] = mx_operand("wo", GROUPS)
         quantise_weights(wo_grouped, wo_q[LAST], 0, COLS)
         new_v1(LAST - 1)
-        regroup_scalar(LAST - 1, 0, SCALAR_COLS)
-        regroup_gpsimd(LAST - 1, SCALAR_COLS, BN)
+        regroup_scalar(LAST - 1, 0, HALF)
+        regroup_gpsimd(LAST - 1, HALF, BN)
+
+        def free_bank():
+            bank = psum_t.tile([P, 2, 2 * P], F32, name="bank_t")
+            return bank[:].rearrange("p h c -> p (h c)")
+
+        acc.append(free_bank())
         for t in range(2, PACK):
-            banks.append(psum_t.tile([P, 2, 2 * P], F32, name="bank_t")[:].rearrange("p h c -> p (h c)"))
+            banks.append(free_bank())
             first_matmul(LAST, t, banks[t])
             gate(LAST, t, banks[t], 0, HALF)
-        second_matmul(LAST - 2, range(PACK))
+        second_matmul(LAST - 3, (2,))
+        second_matmul(LAST - 2, range(PACK - 1))
+        for g in range(DEFERRED):
+            second_matmul(g, (3,))
         new_v1(LAST)
         regroup_scalar(LAST, 0, HALF)
-        v1_q[LAST - 1] = mx_operand("v1", 2)
+        v1_q[LAST - 1] = mx_operand("v1", GROUPS)
         quantise_v1(LAST - 1, 0, BN)
-        second_matmul(LAST - 1, range(PACK))
+        second_matmul(LAST - 1, range(PACK - 1))
         for t in range(PACK):
             gate(LAST, t, banks[t], HALF, BN)
-        v1_q[LAST] = mx_operand("v1", 2)
+        v1_q[LAST] = mx_operand("v1", GROUPS)
         quantise_v1(LAST, 0, HALF)
-        second_matmul(LAST, range(PACK), 0, HALF)
+        second_matmul(LAST, range(PACK - 1), 0, HALF)
         regroup_scalar(LAST, HALF, BN - LAST_VECTOR_COLS)
         regroup_vector(LAST, BN - LAST_VECTOR_COLS, BN)
         quantise_v1(LAST, HALF, BN)
-        second_matmul(LAST, range(PACK), HALF, BN)
+        second_matmul(LAST, range(PACK - 1), HALF, BN)
+        for g in range(DEFERRED, GROUPS):
+            second_matmul(g, (3,))
 
         res = const.tile([P, PACK, BN], F32)
         total = const.tile([P, PACK], F32)
@@ -350,7 +367,7 @@ def tile_nonlocallayer_pa_k_kernel(tc, inputs, Wv, bv, row, Wo, bo, gamma, beta,
         def residual(t):
             nc.vector.scalar_tensor_tensor(
                 out=res[:, t, :],
-                in0=acc[t][:],
+                in0=acc[t],
                 scalar=col(neg_bo, t),
                 in1=x_bo[:, t, :],
                 op0=ALU.max,
@@ -407,14 +424,7 @@ def tile_nonlocallayer_pa_k_kernel(tc, inputs, Wv, bv, row, Wo, bo, gamma, beta,
                 in_=res[:, t, :].rearrange("p (b n) -> p b n", b=B),
             )
 
-        positive = const.tile([P, B, N], F32)
-        nc.scalar.activation(
-            out=positive[:].rearrange("p b n -> p (b n)"), in_=acc[3][:], func=ACT.Relu, bias=chan[:, 0, 3:4]
-        )
         residual(0)
-        nc.gpsimd.tensor_tensor(
-            out=res[:, 3, :].rearrange("p (b n) -> p b n", b=B), in0=positive[:], in1=x_res[:, :, 3, :], op=ALU.add
-        )
         residual(1)
         negative_mean(0)
         squared_deviations(0)
@@ -425,24 +435,25 @@ def tile_nonlocallayer_pa_k_kernel(tc, inputs, Wv, bv, row, Wo, bo, gamma, beta,
         reciprocal_deviation(1, col(sum_square, 1), 1.0 / BN)
         make_gain(0)
         negative_mean(2)
-        nc.vector.bn_stats(out=stats[:], in_=res[:, 3, :])
         make_shift(0)
-        nc.vector.bn_aggr(out=mean_var[:], in_=stats[:])
-        norm_vector(0)
-        store(0)
-        reciprocal_deviation(3, mean_var[:, 1:2], 1.0)
         squared_deviations(2)
         reciprocal_deviation(2, col(sum_square, 2), 1.0 / BN)
+        residual(3)
+        norm_vector(0)
+        store(0)
+        nc.vector.bn_stats(out=stats[:], in_=res[:, 3, :])
         make_gain(1)
-        nc.vector.tensor_scalar(out=col(neg_mean, 3), in0=mean_var[:, 0:1], scalar1=-1.0, scalar2=None, op0=ALU.mult)
+        negative_mean(3)
+        nc.vector.bn_aggr(out=mean_var[:], in_=stats[:])
         make_shift(1)
-        make_gain(3)
+        reciprocal_deviation(3, mean_var[:, 1:2], 1.0)
+        make_gain(2)
         norm_vector(1)
         store(1)
-        make_shift(3)
-        make_gain(2)
-        norm_vector(3)
-        store(3)
         make_shift(2)
         norm_scalar(2)
         store(2)
+        make_gain(3)
+        make_shift(3)
+        norm_vector(3)
+        store(3)

@@ -22,7 +22,7 @@ RUN = 4
 
 COLS = 512
 
-RAW_HALVES = 16
+RAW_HALVES = 12
 
 SCALAR_COLS = 384
 LAST_VECTOR_COLS = 160
@@ -132,10 +132,11 @@ def tile_nonlocallayer_pa_k_kernel(tc, inputs, Wv, bv, row, Wo, bo, gamma, beta,
                 transpose_half(halves[(g, j)], grouped, j)
             return grouped
 
-        def mx_operand(name, bufs):
-            words = work.tile([P, COLS], U32, name=name + "_words", bufs=bufs, align_bytes=64)
-            scales = work.tile([P, COLS], U8, name=name + "_scales", bufs=bufs, align_bytes=64)
-            return words, scales
+        def mx_operand(name, bufs, moving=False):
+            skip_words, skip_scales = (32, 192) if moving else (0, 64)
+            words = work.tile([P, skip_words + COLS], U32, name=name + "_words", bufs=bufs, align_bytes=256)
+            scales = work.tile([P, skip_scales + COLS], U8, name=name + "_scales", bufs=bufs, align_bytes=256)
+            return words[:, skip_words:], scales[:, skip_scales:]
 
         def quantise(values, operand, first, last):
             words, scales = operand
@@ -157,8 +158,8 @@ def tile_nonlocallayer_pa_k_kernel(tc, inputs, Wv, bv, row, Wo, bo, gamma, beta,
                 out=bank,
                 lhsT=words[:, cols].bitcast(FP8X4),
                 lhsT_scale=scales[:, cols],
-                rhs=x_q[0][:].bitcast(FP8X4),
-                rhs_scale=x_q[1][:],
+                rhs=x_q[0].bitcast(FP8X4),
+                rhs_scale=x_q[1],
                 start=True,
                 stop=True,
             )
@@ -221,7 +222,7 @@ def tile_nonlocallayer_pa_k_kernel(tc, inputs, Wv, bv, row, Wo, bo, gamma, beta,
 
         wv_grouped = work.tile([P, COLS, 2], F32, name="wv_grouped", align_bytes=64)
         x_grouped = const.tile([P, B, N, PACK], BF16, align_bytes=64)
-        x_q = mx_operand("x", 1)
+        x_q = mx_operand("x", 1, moving=True)
         wv_q[0] = mx_operand("wv", 2)
 
         def regroup_x(b):
@@ -237,12 +238,12 @@ def tile_nonlocallayer_pa_k_kernel(tc, inputs, Wv, bv, row, Wo, bo, gamma, beta,
         transpose_half(wv_raw[(0, 0)], wv_grouped, 0)
         row_bank = psum_v.tile([P, BN], F32, name="bank_v")
         nc.tensor.matmul(out=row_bank[:], lhsT=share[:], rhs=row_few[:], start=True, stop=True)
-        transpose_half(wv_raw[(0, 1)], wv_grouped, 1)
         row_all = const.tile([P, BN], F32)
+        nc.scalar.copy(out=row_all[:], in_=row_bank[:])
+        transpose_half(wv_raw[(0, 1)], wv_grouped, 1)
         regroup_x(1)
         quantise_weights(wv_grouped, wv_q[0], 0, COLS // 2)
         quantise_x(1)
-        nc.vector.tensor_copy(out=row_all[:], in_=row_bank[:])
 
         chan = const.tile([P, 3, PACK], F32)
         neg_bo = const.tile([P, PACK], F32)
@@ -267,17 +268,20 @@ def tile_nonlocallayer_pa_k_kernel(tc, inputs, Wv, bv, row, Wo, bo, gamma, beta,
         LAST = GROUPS - 1
         for i in range(LAST):
             if 0 <= i - 2:
-                v1_q[i - 2] = mx_operand("v1", GROUPS)
+                v1_q[i - 2] = mx_operand("v1", GROUPS, moving=True)
                 quantise_v1(i - 2, 0, BN)
             new_gated(i)
             if i == 0:
                 wv_grouped_0 = wv_grouped
                 wv_grouped = work.tile([P, COLS, 2], F32, name="wv_grouped", align_bytes=64)
+                wo_grouped = work.tile([P, COLS, 2], F32, name="wo_grouped", align_bytes=64)
                 transpose_half(wv_raw[(1, 0)], wv_grouped, 0)
-                gated_tiles(0, (0, 1))
                 quantise_weights(wv_grouped_0, wv_q[0], COLS // 2, COLS)
+                gated_tiles(0, (0, 1))
                 transpose_half(wv_raw[(1, 1)], wv_grouped, 1)
                 gated_tiles(0, (2, 3))
+                transpose_half(wo_raw[(0, 0)], wo_grouped, 0)
+                transpose_half(wo_raw[(0, 1)], wo_grouped, 1)
             else:
                 wv_grouped = transpose_group(wv_raw, i + 1, "wv_grouped")
                 gated_tiles(i, (0, 1))
@@ -293,8 +297,8 @@ def tile_nonlocallayer_pa_k_kernel(tc, inputs, Wv, bv, row, Wo, bo, gamma, beta,
                 prepare_channels()
             if LAST - 4 <= i:
                 prepare_x(i - (LAST - 4))
-            wo_grouped = transpose_group(wo_raw, i, "wo_grouped")
             if i > 0:
+                wo_grouped = transpose_group(wo_raw, i, "wo_grouped")
                 gated_tiles(i, (2, 3))
             if 0 <= i - 2:
                 second_matmul(i - 2, (0, 1))
@@ -304,7 +308,7 @@ def tile_nonlocallayer_pa_k_kernel(tc, inputs, Wv, bv, row, Wo, bo, gamma, beta,
                 regroup_scalar(i - 1, SCALAR_COLS // 2, SCALAR_COLS)
 
         HALF = BN // 2
-        v1_q[LAST - 2] = mx_operand("v1", GROUPS)
+        v1_q[LAST - 2] = mx_operand("v1", GROUPS, moving=True)
         quantise_v1(LAST - 2, 0, BN)
         wo_grouped = transpose_group(wo_raw, LAST, "wo_grouped")
         new_gated(LAST)
@@ -335,12 +339,12 @@ def tile_nonlocallayer_pa_k_kernel(tc, inputs, Wv, bv, row, Wo, bo, gamma, beta,
             second_matmul(g, (3,))
         new_v1(LAST)
         regroup_scalar(LAST, 0, HALF)
-        v1_q[LAST - 1] = mx_operand("v1", GROUPS)
+        v1_q[LAST - 1] = mx_operand("v1", GROUPS, moving=True)
         quantise_v1(LAST - 1, 0, BN)
         second_matmul(LAST - 1, range(PACK - 1))
         for t in range(PACK):
             gate(LAST, t, banks[t], HALF, BN)
-        v1_q[LAST] = mx_operand("v1", GROUPS)
+        v1_q[LAST] = mx_operand("v1", GROUPS, moving=True)
         quantise_v1(LAST, 0, HALF)
         second_matmul(LAST, range(PACK - 1), 0, HALF)
         regroup_scalar(LAST, HALF, BN - LAST_VECTOR_COLS)
@@ -356,8 +360,8 @@ def tile_nonlocallayer_pa_k_kernel(tc, inputs, Wv, bv, row, Wo, bo, gamma, beta,
         square = const.tile([P, BN], F32)
         sum_square = const.tile([P, PACK], F32)
         rstd = const.tile([P, PACK], F32)
-        stats = const.tile([P, 6], F32)
-        mean_var = const.tile([P, 2], F32)
+        stats = const.tile([P, 2, 6], F32)
+        mean_var = const.tile([P, 2, 2], F32)
         gain = const.tile([P, PACK], F32)
         shift = const.tile([P, PACK], F32)
 
@@ -385,9 +389,9 @@ def tile_nonlocallayer_pa_k_kernel(tc, inputs, Wv, bv, row, Wo, bo, gamma, beta,
                 out=square[:], in_=res[:, t, :], func=ACT.Square, bias=col(neg_mean, t), accum_out=col(sum_square, t)
             )
 
-        def reciprocal_deviation(t, variance, scale):
+        def reciprocal_deviation(t):
             nc.scalar.activation(
-                out=col(rstd, t), in_=variance, func=ACT.Abs_reciprocal_sqrt, scale=scale, bias=eps[:, 0:1]
+                out=col(rstd, t), in_=col(sum_square, t), func=ACT.Abs_reciprocal_sqrt, scale=1.0 / BN, bias=eps[:, 0:1]
             )
 
         def make_gain(t):
@@ -425,35 +429,38 @@ def tile_nonlocallayer_pa_k_kernel(tc, inputs, Wv, bv, row, Wo, bo, gamma, beta,
             )
 
         residual(0)
-        residual(1)
         negative_mean(0)
         squared_deviations(0)
-        reciprocal_deviation(0, col(sum_square, 0), 1.0 / BN)
-        residual(2)
+        reciprocal_deviation(0)
+        residual(1)
         negative_mean(1)
         squared_deviations(1)
-        reciprocal_deviation(1, col(sum_square, 1), 1.0 / BN)
+        reciprocal_deviation(1)
+        residual(2)
         make_gain(0)
-        negative_mean(2)
-        make_shift(0)
-        squared_deviations(2)
-        reciprocal_deviation(2, col(sum_square, 2), 1.0 / BN)
         residual(3)
-        norm_vector(0)
+        make_shift(0)
+        norm_scalar(0)
         store(0)
-        nc.vector.bn_stats(out=stats[:], in_=res[:, 3, :])
         make_gain(1)
-        negative_mean(3)
-        nc.vector.bn_aggr(out=mean_var[:], in_=stats[:])
+        nc.vector.bn_stats(out=stats[:, 0, :], in_=res[:, 2, :])
         make_shift(1)
-        reciprocal_deviation(3, mean_var[:, 1:2], 1.0)
-        make_gain(2)
-        norm_vector(1)
+        norm_scalar(1)
         store(1)
+        nc.vector.bn_stats(out=stats[:, 1, :], in_=res[:, 3, :])
+        for i in range(2):
+            nc.vector.bn_aggr(out=mean_var[:, i, :], in_=stats[:, i, :])
+        pair = slice(2, PACK)
+        nc.scalar.activation(
+            out=rstd[:, pair], in_=mean_var[:, :, 1], func=ACT.Abs_reciprocal_sqrt, bias=eps[:, 0:1]
+        )
+        nc.vector.tensor_scalar(
+            out=neg_mean[:, pair], in0=mean_var[:, :, 0], scalar1=-1.0, scalar2=None, op0=ALU.mult
+        )
+        nc.vector.tensor_tensor(out=gain[:, pair], in0=rstd[:, pair], in1=chan[:, 1, pair], op=ALU.mult)
         make_shift(2)
+        make_shift(3)
         norm_scalar(2)
         store(2)
-        make_gain(3)
-        make_shift(3)
         norm_vector(3)
         store(3)

@@ -211,10 +211,11 @@ def tile_nonlocallayer_pa_k_kernel(tc, inputs, Wv, bv, row, Wo, bo, gamma, beta,
             quantise(v1[g][:, first:last, :].rearrange("p c t -> p (c t)"), v1_q[g], first, last)
 
         wv_q, wo_q, v1_q, gated, v1 = {}, {}, {}, {}, {}
-        acc = []
-        for t in range(PACK - 1):
+        early = []
+        for t in range(2):
             bank = psum_o.tile([P, BN], F32, name="acc%d" % t)
-            acc.append(bank[:])
+            early.append(bank[:])
+        acc = []
 
         bv_bank = psum_v.tile([P, BN], F32, name="bank_v")
         nc.tensor.transpose(bv_bank[:, 0:P], bv_rows[:].bitcast(F32), ident[:])
@@ -271,6 +272,10 @@ def tile_nonlocallayer_pa_k_kernel(tc, inputs, Wv, bv, row, Wo, bo, gamma, beta,
                 v1_q[i - 2] = mx_operand("v1", GROUPS, moving=True)
                 quantise_v1(i - 2, 0, BN)
             new_gated(i)
+            if i == 1:
+                for t in range(PACK - 1):
+                    bank = psum_o.tile([P, BN], F32, name="acc%d" % t)
+                    acc.append(bank[:])
             if i == 0:
                 wv_grouped_0 = wv_grouped
                 wv_grouped = work.tile([P, COLS, 2], F32, name="wv_grouped", align_bytes=64)
@@ -278,10 +283,12 @@ def tile_nonlocallayer_pa_k_kernel(tc, inputs, Wv, bv, row, Wo, bo, gamma, beta,
                 transpose_half(wv_raw[(1, 0)], wv_grouped, 0)
                 quantise_weights(wv_grouped_0, wv_q[0], COLS // 2, COLS)
                 gated_tiles(0, (0, 1))
+                for t in (2, 3):
+                    first_matmul(0, t, early[t - 2])
+                    gate(0, t, early[t - 2], 0, BN)
                 transpose_half(wv_raw[(1, 1)], wv_grouped, 1)
-                gated_tiles(0, (2, 3))
-                transpose_half(wo_raw[(0, 0)], wo_grouped, 0)
-                transpose_half(wo_raw[(0, 1)], wo_grouped, 1)
+                for j in range(2):
+                    transpose_half(wo_raw[(0, j)], wo_grouped, j)
             else:
                 wv_grouped = transpose_group(wv_raw, i + 1, "wv_grouped")
                 gated_tiles(i, (0, 1))
@@ -360,8 +367,8 @@ def tile_nonlocallayer_pa_k_kernel(tc, inputs, Wv, bv, row, Wo, bo, gamma, beta,
         square = const.tile([P, BN], F32)
         sum_square = const.tile([P, PACK], F32)
         rstd = const.tile([P, PACK], F32)
-        stats = const.tile([P, 2, 6], F32)
-        mean_var = const.tile([P, 2, 2], F32)
+        stats = const.tile([P, 6], F32)
+        mean_var = const.tile([P, 2], F32)
         gain = const.tile([P, PACK], F32)
         shift = const.tile([P, PACK], F32)
 
@@ -384,15 +391,16 @@ def tile_nonlocallayer_pa_k_kernel(tc, inputs, Wv, bv, row, Wo, bo, gamma, beta,
                 out=col(neg_mean, t), in0=col(total, t), scalar1=-1.0 / BN, scalar2=None, op0=ALU.mult
             )
 
+        def reciprocal_deviation(t, total_square, scale):
+            nc.scalar.activation(
+                out=col(rstd, t), in_=total_square, func=ACT.Abs_reciprocal_sqrt, scale=scale, bias=eps[:, 0:1]
+            )
+
         def squared_deviations(t):
             nc.scalar.activation(
                 out=square[:], in_=res[:, t, :], func=ACT.Square, bias=col(neg_mean, t), accum_out=col(sum_square, t)
             )
-
-        def reciprocal_deviation(t):
-            nc.scalar.activation(
-                out=col(rstd, t), in_=col(sum_square, t), func=ACT.Abs_reciprocal_sqrt, scale=1.0 / BN, bias=eps[:, 0:1]
-            )
+            reciprocal_deviation(t, col(sum_square, t), 1.0 / BN)
 
         def make_gain(t):
             nc.vector.tensor_tensor(out=col(gain, t), in0=col(rstd, t), in1=chan[:, 1, t : t + 1], op=ALU.mult)
@@ -431,36 +439,30 @@ def tile_nonlocallayer_pa_k_kernel(tc, inputs, Wv, bv, row, Wo, bo, gamma, beta,
         residual(0)
         negative_mean(0)
         squared_deviations(0)
-        reciprocal_deviation(0)
         residual(1)
         negative_mean(1)
         squared_deviations(1)
-        reciprocal_deviation(1)
         residual(2)
         make_gain(0)
         residual(3)
         make_shift(0)
-        norm_scalar(0)
-        store(0)
+        negative_mean(3)
+        squared_deviations(3)
         make_gain(1)
-        nc.vector.bn_stats(out=stats[:, 0, :], in_=res[:, 2, :])
+        nc.vector.bn_stats(out=stats[:], in_=res[:, 2, :])
         make_shift(1)
-        norm_scalar(1)
+        norm_vector(0)
+        store(0)
+        nc.vector.bn_aggr(out=mean_var[:], in_=stats[:])
+        reciprocal_deviation(2, mean_var[:, 1:2], 1.0)
+        norm_vector(1)
         store(1)
-        nc.vector.bn_stats(out=stats[:, 1, :], in_=res[:, 3, :])
-        for i in range(2):
-            nc.vector.bn_aggr(out=mean_var[:, i, :], in_=stats[:, i, :])
-        pair = slice(2, PACK)
-        nc.scalar.activation(
-            out=rstd[:, pair], in_=mean_var[:, :, 1], func=ACT.Abs_reciprocal_sqrt, bias=eps[:, 0:1]
-        )
-        nc.vector.tensor_scalar(
-            out=neg_mean[:, pair], in0=mean_var[:, :, 0], scalar1=-1.0, scalar2=None, op0=ALU.mult
-        )
-        nc.vector.tensor_tensor(out=gain[:, pair], in0=rstd[:, pair], in1=chan[:, 1, pair], op=ALU.mult)
-        make_shift(2)
+        negative_mean(2)
+        make_gain(3)
+        make_gain(2)
         make_shift(3)
-        norm_scalar(2)
-        store(2)
+        make_shift(2)
         norm_vector(3)
         store(3)
+        norm_scalar(2)
+        store(2)

@@ -100,6 +100,8 @@ def tile_nonlocallayer_pa_k_kernel(tc, inputs, Wv, bv, row, Wo, bo, gamma, beta,
         for k, vec in enumerate((bo, gamma, beta)):
             nc.sync.dma_start(out=chan_bf[:, k, 0:PACK], in_=vec.rearrange("(p t) -> p t", t=PACK))
 
+        zeros = const.tile([P, BN], BF16)
+        nc.vector.memset(zeros[:], 0.0)
         eps = const.tile([P, 1], F32)
         nc.vector.memset(eps[:], BN_EPS)
 
@@ -117,6 +119,10 @@ def tile_nonlocallayer_pa_k_kernel(tc, inputs, Wv, bv, row, Wo, bo, gamma, beta,
             nc.vector.memset(row_few[lo:hi, :], 0.0)
         warm = const.tile([P, 1], F32)
         nc.scalar.activation(out=warm[:], in_=eps[:], func=ACT.Abs_reciprocal_sqrt)
+
+        def keep_clock(count):
+            for i in range(count):
+                nc.tensor.matmul(out=warm_bank, lhsT=zeros[:, 0:P], rhs=zeros[:], start=True, stop=True)
 
         def transpose_half(rows, grouped, j):
             bank = psum_t.tile([P, 2, 2 * P], F32, name="bank_t")
@@ -217,6 +223,10 @@ def tile_nonlocallayer_pa_k_kernel(tc, inputs, Wv, bv, row, Wo, bo, gamma, beta,
             early.append(bank[:])
         acc = []
 
+        warm_tile = psum_o.tile([P, BN], F32, name="acc2")
+        warm_bank = warm_tile[:]
+        keep_clock(3)
+
         bv_bank = psum_v.tile([P, BN], F32, name="bank_v")
         nc.tensor.transpose(bv_bank[:, 0:P], bv_rows[:].bitcast(F32), ident[:])
         bv_f32 = const.tile([P, PACK * GROUPS], F32)
@@ -236,11 +246,13 @@ def tile_nonlocallayer_pa_k_kernel(tc, inputs, Wv, bv, row, Wo, bo, gamma, beta,
         regroup_x(0)
         nc.vector.tensor_copy(out=bv_f32[:], in_=bv_bank[:, 0 : 2 * GROUPS].bitcast(BF16))
         quantise_x(0)
+        keep_clock(1)
         transpose_half(wv_raw[(0, 0)], wv_grouped, 0)
         row_bank = psum_v.tile([P, BN], F32, name="bank_v")
         nc.tensor.matmul(out=row_bank[:], lhsT=share[:], rhs=row_few[:], start=True, stop=True)
         row_all = const.tile([P, BN], F32)
         nc.scalar.copy(out=row_all[:], in_=row_bank[:])
+        keep_clock(1)
         transpose_half(wv_raw[(0, 1)], wv_grouped, 1)
         regroup_x(1)
         quantise_weights(wv_grouped, wv_q[0], 0, COLS // 2)
@@ -273,9 +285,12 @@ def tile_nonlocallayer_pa_k_kernel(tc, inputs, Wv, bv, row, Wo, bo, gamma, beta,
                 quantise_v1(i - 2, 0, BN)
             new_gated(i)
             if i == 1:
-                for t in range(PACK - 1):
+                for t in range(2):
                     bank = psum_o.tile([P, BN], F32, name="acc%d" % t)
                     acc.append(bank[:])
+            if i == 3:
+                bank = psum_o.tile([P, BN], F32, name="acc2")
+                acc.append(bank[:])
             if i == 0:
                 wv_grouped_0 = wv_grouped
                 wv_grouped = work.tile([P, COLS, 2], F32, name="wv_grouped", align_bytes=64)
@@ -292,6 +307,8 @@ def tile_nonlocallayer_pa_k_kernel(tc, inputs, Wv, bv, row, Wo, bo, gamma, beta,
             else:
                 wv_grouped = transpose_group(wv_raw, i + 1, "wv_grouped")
                 gated_tiles(i, (0, 1))
+                if i <= 2:
+                    keep_clock(1)
             if 0 <= i - 3:
                 second_matmul(i - 3, (2,))
             wv_q[i + 1] = mx_operand("wv", 2)
@@ -307,6 +324,8 @@ def tile_nonlocallayer_pa_k_kernel(tc, inputs, Wv, bv, row, Wo, bo, gamma, beta,
             if i > 0:
                 wo_grouped = transpose_group(wo_raw, i, "wo_grouped")
                 gated_tiles(i, (2, 3))
+                if i == 1:
+                    keep_clock(1)
             if 0 <= i - 2:
                 second_matmul(i - 2, (0, 1))
             wo_q[i] = mx_operand("wo", GROUPS)

from contextlib import ExitStack

import concourse.masks as masks
import concourse.mybir as mybir

F32 = mybir.dt.float32
BF16 = mybir.dt.bfloat16
U32 = mybir.dt.uint32
U8 = mybir.dt.uint8
FP8X4 = mybir.dt.float8_e4m3fn_x4
ALU = mybir.AluOpType
ACT = mybir.ActivationFunctionType

P = 128
PACK = 4
K_PASS = P * PACK
B, C, F, N = 2, 512, 8192, 256
BN = B * N
GROUPS = F // K_PASS
BN_EPS = 1e-5
RUN = 4

COLS = 512

RAW_HALVES = 12

SCALAR_COLS = 384
LAST_VECTOR_COLS = 160
DEFERRED = 8
BF16_TOP = 3.4e38

FLOPS = 2 * (2 * F * C * BN)


def side_by_side(rows, grouped):
    return (
        rows.rearrange("p t (c i) -> p c t i", i=RUN),
        grouped.rearrange("p (c i) t -> p c t i", i=RUN),
    )


def tile_nonlocallayer_pa_k_kernel(tc, inputs, Wv, bv, row, Wo, bo, gamma, beta, out):
    nc = tc.nc
    x_dram = inputs.rearrange("b c t h w -> b c (t h w)")
    y_dram = out.rearrange("b c t h w -> b c (t h w)")

    with ExitStack() as ctx:
        const = ctx.enter_context(tc.tile_pool(name="const", bufs=1))
        raw = ctx.enter_context(tc.tile_pool(name="raw", bufs=RAW_HALVES))
        work = ctx.enter_context(tc.tile_pool(name="work", bufs=2))
        psum_t = ctx.enter_context(tc.psum_pool(name="psum_t", bufs=3))
        psum_v = ctx.enter_context(tc.psum_pool(name="psum_v", bufs=2))
        psum_o = ctx.enter_context(tc.psum_pool(name="psum_o", bufs=1))
        ctx.enter_context(tc.manual_schedule())

        def load_wv(g, u):
            first = g * K_PASS + u * 2 * P
            t = raw.tile([P, 2, C], BF16, name="wv_raw")
            nc.sync.dma_start(
                out=t[:].rearrange("r e c -> r (e c)"),
                in_=Wv[first : first + 2 * P, :].rearrange("(r e) c -> r (e c)", e=2),
            )
            return t

        def load_wo(g, j):
            t = raw.tile([P, 2, K_PASS], BF16, name="wo_raw")
            nc.sync.dma_start(
                out=t[:],
                in_=Wo[:, g * K_PASS : (g + 1) * K_PASS].rearrange("(r t) f -> r t f", t=PACK)[:, 2 * j : 2 * j + 2, :],
            )
            return t

        x_rows = const.tile([P, B, PACK, N], BF16)

        def load_x(b):
            nc.sync.dma_start(
                out=x_rows[:, b].rearrange("p (h e) n -> p h (e n)", e=2),
                in_=x_dram[b].rearrange("(h p e) n -> p h (e n)", h=2, e=2),
            )

        wv_raw = {}
        load_x(0)
        wv_raw[(0, 0)] = load_wv(0, 0)
        load_x(1)
        wv_raw[(0, 1)] = load_wv(0, 1)
        wo_raw = {}
        for g in range(GROUPS):
            for half in range(2):
                if g + 1 < GROUPS:
                    wv_raw[(g + 1, half)] = load_wv(g + 1, half)
            for half in range(2):
                wo_raw[(g, half)] = load_wo(g, half)
        x_res = const.tile([P, B, PACK, N], BF16)
        for b in range(B):
            nc.sync.dma_start(
                out=x_res[:, b].rearrange("p t n -> p (t n)"),
                in_=x_dram[b].rearrange("(p t) n -> p (t n)", t=PACK),
            )
        chan_bf = const.tile([P, 3, 16], BF16)
        for k, vec in enumerate((bo, gamma, beta)):
            nc.sync.dma_start(out=chan_bf[:, k, 0:PACK], in_=vec.rearrange("(p t) -> p t", t=PACK))

        zeros = const.tile([P, BN], BF16)
        nc.vector.memset(zeros[:], 0.0)
        eps = const.tile([P, 1], F32)
        nc.vector.memset(eps[:], BN_EPS)

        ident = const.tile([P, P], F32)
        masks.make_identity(nc, ident[:])

        bv_rows = const.tile([P, 2 * P], BF16)
        nc.scalar.dma_start(out=bv_rows[0 : 2 * GROUPS, :], in_=bv.rearrange("(j w) -> j w", w=2 * P))
        row_few = const.tile([P, BN], BF16)
        nc.scalar.dma_start(out=row_few[0:32, :], in_=row.rearrange("b n -> (b n)").partition_broadcast(32))
        share = const.tile([P, P], BF16)
        nc.vector.memset(share[:], 1.0 / 32)
        for lo, hi in ((32, 64), (64, P)):
            nc.vector.memset(bv_rows[lo:hi, :], 0.0)
            nc.vector.memset(row_few[lo:hi, :], 0.0)
        warm = const.tile([P, 1], F32)
        nc.scalar.activation(out=warm[:], in_=eps[:], func=ACT.Abs_reciprocal_sqrt)

        def keep_clock(count):
            for i in range(count):
                nc.tensor.matmul(out=warm_bank, lhsT=zeros[:, 0:P], rhs=zeros[:], start=True, stop=True)

        def transpose_half(rows, grouped, j):
            bank = psum_t.tile([P, 2, 2 * P], F32, name="bank_t")
            for i in range(2):
                words = rows[:, i, :].bitcast(F32)
                for h in range(2):
                    nc.tensor.transpose(bank[:, h, i * P : (i + 1) * P], words[:, h * P : (h + 1) * P], ident[:])
            nc.scalar.copy(out=grouped[:, 2 * j * P : 2 * (j + 1) * P, :], in_=bank[:].rearrange("p h c -> p c h"))

        def transpose_group(halves, g, name):
            grouped = work.tile([P, COLS, 2], F32, name=name, align_bytes=64)
            for j in range(2):
                transpose_half(halves[(g, j)], grouped, j)
            return grouped

        def mx_operand(name, bufs, moving=False):
            skip_words, skip_scales = (32, 192) if moving else (0, 64)
            words = work.tile([P, skip_words + COLS], U32, name=name + "_words", bufs=bufs, align_bytes=256)
            scales = work.tile([P, skip_scales + COLS], U8, name=name + "_scales", bufs=bufs, align_bytes=256)
            return words[:, skip_words:], scales[:, skip_scales:]

        def quantise(values, operand, first, last):
            words, scales = operand
            nc.vector.quantize_mx(out=words[:, first:last].bitcast(FP8X4), scales=scales[:, first:last], in_=values)

        def new_gated(g):
            gated[g] = work.tile([P, PACK, BN], BF16, name="gated")

        def new_v1(g):
            v1[g] = work.tile([P, BN, PACK], BF16, name="v1", align_bytes=64)

        def quantise_weights(grouped, operand, first, last):
            quantise(grouped[:, first:last, :].rearrange("p c h -> p (c h)").bitcast(BF16), operand, first, last)

        def first_matmul(g, t, bank):
            words, scales = wv_q[g]
            cols = slice(t * P, (t + 1) * P)
            nc.tensor.matmul_mx(
                out=bank,
                lhsT=words[:, cols].bitcast(FP8X4),
                lhsT_scale=scales[:, cols],
                rhs=x_q[0].bitcast(FP8X4),
                rhs_scale=x_q[1],
                start=True,
                stop=True,
            )

        def gate(g, t, bank, first, last):
            nc.vector.scalar_tensor_tensor(
                out=gated[g][:, t, first:last],
                in0=bank[:, first:last],
                scalar=bv_f32[:, PACK * g + t : PACK * g + t + 1],
                in1=row_all[:, first:last],
                op0=ALU.add,
                op1=ALU.mult,
            )

        def gated_tiles(g, tiles):
            for t in tiles:
                bank = psum_v.tile([P, BN], F32, name="bank_v")
                first_matmul(g, t, bank[:])
                gate(g, t, bank, 0, BN)

        def second_matmul(g, tiles, first=0, last=BN):
            w_words, w_scales = wo_q[g]
            v_words, v_scales = v1_q[g]
            for t in tiles:
                cols = slice(t * P, (t + 1) * P)
                nc.tensor.matmul_mx(
                    out=acc[t][:, first:last],
                    lhsT=w_words[:, cols].bitcast(FP8X4),
                    lhsT_scale=w_scales[:, cols],
                    rhs=v_words[:, first:last].bitcast(FP8X4),
                    rhs_scale=v_scales[:, first:last],
                    start=(g == 0),
                    stop=(g == GROUPS - 1 and last == BN),
                )

        def regroup_scalar(g, first, last):
            src, dst = side_by_side(gated[g][:, :, first:last], v1[g][:, first:last, :])
            nc.scalar.activation(out=dst, in_=src, func=ACT.Relu)

        def regroup_gpsimd(g, first, last):
            src, dst = side_by_side(gated[g][:, :, first:last], v1[g][:, first:last, :])
            nc.gpsimd.tensor_scalar(out=dst, in0=src, scalar1=BF16_TOP, scalar2=0.0, op0=ALU.min, op1=ALU.max)

        def regroup_vector(g, first, last):
            src, dst = side_by_side(gated[g][:, :, first:last], v1[g][:, first:last, :])
            nc.vector.tensor_scalar_max(out=dst, in0=src, scalar1=0.0)

        def quantise_v1(g, first, last):
            quantise(v1[g][:, first:last, :].rearrange("p c t -> p (c t)"), v1_q[g], first, last)

        wv_q, wo_q, v1_q, gated, v1 = {}, {}, {}, {}, {}
        early = []
        for t in range(2):
            bank = psum_o.tile([P, BN], F32, name="acc%d" % t)
            early.append(bank[:])
        acc = []

        warm_tile = psum_o.tile([P, BN], F32, name="acc2")
        warm_bank = warm_tile[:]
        keep_clock(3)

        bv_bank = psum_v.tile([P, BN], F32, name="bank_v")
        nc.tensor.transpose(bv_bank[:, 0:P], bv_rows[:].bitcast(F32), ident[:])
        bv_f32 = const.tile([P, PACK * GROUPS], F32)

        wv_grouped = work.tile([P, COLS, 2], F32, name="wv_grouped", align_bytes=64)
        x_grouped = const.tile([P, B, N, PACK], BF16, align_bytes=64)
        x_q = mx_operand("x", 1, moving=True)
        wv_q[0] = mx_operand("wv", 2)

        def regroup_x(b):
            src, dst = side_by_side(x_rows[:, b], x_grouped[:, b])
            nc.vector.tensor_copy(out=dst, in_=src)

        def quantise_x(b):
            quantise(x_grouped[:, b].rearrange("p n t -> p (n t)"), x_q, b * N, (b + 1) * N)

        regroup_x(0)
        nc.vector.tensor_copy(out=bv_f32[:], in_=bv_bank[:, 0 : 2 * GROUPS].bitcast(BF16))
        quantise_x(0)
        keep_clock(1)
        transpose_half(wv_raw[(0, 0)], wv_grouped, 0)
        row_bank = psum_v.tile([P, BN], F32, name="bank_v")
        nc.tensor.matmul(out=row_bank[:], lhsT=share[:], rhs=row_few[:], start=True, stop=True)
        row_all = const.tile([P, BN], F32)
        nc.scalar.copy(out=row_all[:], in_=row_bank[:])
        keep_clock(1)
        transpose_half(wv_raw[(0, 1)], wv_grouped, 1)
        regroup_x(1)
        quantise_weights(wv_grouped, wv_q[0], 0, COLS // 2)
        quantise_x(1)

        chan = const.tile([P, 3, PACK], F32)
        neg_bo = const.tile([P, PACK], F32)
        x_bo = const.tile([P, PACK, BN], F32)

        def prepare_channels():
            nc.gpsimd.tensor_copy(out=chan[:], in_=chan_bf[:, :, 0:PACK])
            nc.gpsimd.tensor_scalar(
                out=neg_bo[:], in0=chan[:, 0, :], scalar1=-1.0, scalar2=0.0, op0=ALU.mult, op1=ALU.add
            )

        def prepare_x(t):
            nc.gpsimd.tensor_scalar(
                out=x_bo[:, t, :].rearrange("p (b n) -> p b n", b=B),
                in0=x_res[:, :, t, :],
                scalar1=1.0,
                scalar2=chan[:, 0, t : t + 1],
                op0=ALU.mult,
                op1=ALU.add,
            )

        LAST = GROUPS - 1
        for i in range(LAST):
            if 0 <= i - 2:
                v1_q[i - 2] = mx_operand("v1", GROUPS, moving=True)
                quantise_v1(i - 2, 0, BN)
            new_gated(i)
            if i == 1:
                for t in range(2):
                    bank = psum_o.tile([P, BN], F32, name="acc%d" % t)
                    acc.append(bank[:])
            if i == 3:
                bank = psum_o.tile([P, BN], F32, name="acc2")
                acc.append(bank[:])
            if i == 0:
                wv_grouped_0 = wv_grouped
                wv_grouped = work.tile([P, COLS, 2], F32, name="wv_grouped", align_bytes=64)
                wo_grouped = work.tile([P, COLS, 2], F32, name="wo_grouped", align_bytes=64)
                transpose_half(wv_raw[(1, 0)], wv_grouped, 0)
                quantise_weights(wv_grouped_0, wv_q[0], COLS // 2, COLS)
                gated_tiles(0, (0, 1))
                for t in (2, 3):
                    first_matmul(0, t, early[t - 2])
                    gate(0, t, early[t - 2], 0, BN)
                transpose_half(wv_raw[(1, 1)], wv_grouped, 1)
                for j in range(2):
                    transpose_half(wo_raw[(0, j)], wo_grouped, j)
            else:
                wv_grouped = transpose_group(wv_raw, i + 1, "wv_grouped")
                gated_tiles(i, (0, 1))
                if i <= 2:
                    keep_clock(1)
            if 0 <= i - 3:
                second_matmul(i - 3, (2,))
            wv_q[i + 1] = mx_operand("wv", 2)
            quantise_weights(wv_grouped, wv_q[i + 1], 0, COLS)
            if 0 <= i - 1:
                new_v1(i - 1)
                regroup_scalar(i - 1, 0, SCALAR_COLS // 2)
                regroup_gpsimd(i - 1, SCALAR_COLS, BN)
            if i == LAST - 5:
                prepare_channels()
            if LAST - 4 <= i:
                prepare_x(i - (LAST - 4))
            if i > 0:
                wo_grouped = transpose_group(wo_raw, i, "wo_grouped")
                gated_tiles(i, (2, 3))
                if i == 1:
                    keep_clock(1)
            if 0 <= i - 2:
                second_matmul(i - 2, (0, 1))
            wo_q[i] = mx_operand("wo", GROUPS)
            quantise_weights(wo_grouped, wo_q[i], 0, COLS)
            if 0 <= i - 1:
                regroup_scalar(i - 1, SCALAR_COLS // 2, SCALAR_COLS)

        HALF = BN // 2
        v1_q[LAST - 2] = mx_operand("v1", GROUPS, moving=True)
        quantise_v1(LAST - 2, 0, BN)
        wo_grouped = transpose_group(wo_raw, LAST, "wo_grouped")
        new_gated(LAST)
        banks = []
        for t in range(2):
            bank = psum_v.tile([P, BN], F32, name="bank_v")
            banks.append(bank[:])
            first_matmul(LAST, t, banks[t])
            gate(LAST, t, banks[t], 0, HALF)
        wo_q[LAST] = mx_operand("wo", GROUPS)
        quantise_weights(wo_grouped, wo_q[LAST], 0, COLS)
        new_v1(LAST - 1)
        regroup_scalar(LAST - 1, 0, HALF)
        regroup_gpsimd(LAST - 1, HALF, BN)

        def free_bank():
            bank = psum_t.tile([P, 2, 2 * P], F32, name="bank_t")
            return bank[:].rearrange("p h c -> p (h c)")

        acc.append(free_bank())
        for t in range(2, PACK):
            banks.append(free_bank())
            first_matmul(LAST, t, banks[t])
            gate(LAST, t, banks[t], 0, HALF)
        second_matmul(LAST - 3, (2,))
        second_matmul(LAST - 2, range(PACK - 1))
        for g in range(DEFERRED):
            second_matmul(g, (3,))
        new_v1(LAST)
        regroup_scalar(LAST, 0, HALF)
        v1_q[LAST - 1] = mx_operand("v1", GROUPS, moving=True)
        quantise_v1(LAST - 1, 0, BN)
        second_matmul(LAST - 1, range(PACK - 1))
        for t in range(PACK):
            gate(LAST, t, banks[t], HALF, BN)
        v1_q[LAST] = mx_operand("v1", GROUPS, moving=True)
        quantise_v1(LAST, 0, HALF)
        second_matmul(LAST, range(PACK - 1), 0, HALF)
        regroup_scalar(LAST, HALF, BN - LAST_VECTOR_COLS)
        regroup_vector(LAST, BN - LAST_VECTOR_COLS, BN)
        quantise_v1(LAST, HALF, BN)
        second_matmul(LAST, range(PACK - 1), HALF, BN)
        for g in range(DEFERRED, GROUPS):
            second_matmul(g, (3,))

        res = const.tile([P, PACK, BN], F32)
        total = const.tile([P, PACK], F32)
        neg_mean = const.tile([P, PACK], F32)
        square = const.tile([P, BN], F32)
        sum_square = const.tile([P, PACK], F32)
        rstd = const.tile([P, PACK], F32)
        stats = const.tile([P, 6], F32)
        mean_var = const.tile([P, 2], F32)
        gain = const.tile([P, PACK], F32)
        shift = const.tile([P, PACK], F32)

        def col(tile, t):
            return tile[:, t : t + 1]

        def residual(t):
            nc.vector.scalar_tensor_tensor(
                out=res[:, t, :],
                in0=acc[t],
                scalar=col(neg_bo, t),
                in1=x_bo[:, t, :],
                op0=ALU.max,
                op1=ALU.add,
                accum_out=col(total, t),
            )

        def negative_mean(t):
            nc.vector.tensor_scalar(
                out=col(neg_mean, t), in0=col(total, t), scalar1=-1.0 / BN, scalar2=None, op0=ALU.mult
            )

        def reciprocal_deviation(t, total_square, scale):
            nc.scalar.activation(
                out=col(rstd, t), in_=total_square, func=ACT.Abs_reciprocal_sqrt, scale=scale, bias=eps[:, 0:1]
            )

        def squared_deviations(t):
            nc.scalar.activation(
                out=square[:], in_=res[:, t, :], func=ACT.Square, bias=col(neg_mean, t), accum_out=col(sum_square, t)
            )
            reciprocal_deviation(t, col(sum_square, t), 1.0 / BN)

        def make_gain(t):
            nc.vector.tensor_tensor(out=col(gain, t), in0=col(rstd, t), in1=chan[:, 1, t : t + 1], op=ALU.mult)

        def make_shift(t):
            nc.vector.tensor_scalar(
                out=col(shift, t),
                in0=col(neg_mean, t),
                scalar1=col(gain, t),
                scalar2=chan[:, 2, t : t + 1],
                op0=ALU.mult,
                op1=ALU.add,
            )

        def norm_vector(t):
            nc.vector.tensor_scalar(
                out=res[:, t, :],
                in0=res[:, t, :],
                scalar1=col(gain, t),
                scalar2=col(shift, t),
                op0=ALU.mult,
                op1=ALU.add,
            )

        def norm_scalar(t):
            nc.scalar.activation(
                out=res[:, t, :], in_=res[:, t, :], func=ACT.Identity, scale=col(gain, t), bias=col(shift, t)
            )

        def store(t):
            nc.sync.dma_start(
                out=y_dram.rearrange("b (p t) n -> t p b n", t=PACK)[t],
                in_=res[:, t, :].rearrange("p (b n) -> p b n", b=B),
            )

        residual(0)
        negative_mean(0)
        squared_deviations(0)
        residual(1)
        negative_mean(1)
        squared_deviations(1)
        residual(2)
        make_gain(0)
        residual(3)
        make_shift(0)
        negative_mean(3)
        squared_deviations(3)
        make_gain(1)
        nc.vector.bn_stats(out=stats[:], in_=res[:, 2, :])
        make_shift(1)
        norm_vector(0)
        store(0)
        nc.vector.bn_aggr(out=mean_var[:], in_=stats[:])
        reciprocal_deviation(2, mean_var[:, 1:2], 1.0)
        norm_vector(1)
        store(1)
        negative_mean(2)
        make_gain(3)
        make_gain(2)
        make_shift(3)
        make_shift(2)
        norm_vector(3)
        store(3)
        norm_scalar(2)
        store(2)
